import numpy as np
import ml_dtypes


def mxq(x, axis, fmt="e4m3"):
    dtype, down = {"e4m3": (ml_dtypes.float8_e4m3fn, 7), "e5m2": (ml_dtypes.float8_e5m2, 14)}[fmt]
    v = np.moveaxis(np.asarray(x, np.float32).astype(ml_dtypes.bfloat16).astype(np.float64), axis, -1)
    blocks = v.reshape(v.shape[:-1] + (-1, 32))
    amax = np.abs(blocks).max(-1, keepdims=True)
    byte = np.maximum(np.where(amax > 0, np.frexp(amax)[1] - 1 + 127, 0) - down, 1)
    scale = np.exp2(byte - 127.0)
    codes = (blocks / scale).astype(np.float32).astype(dtype).astype(np.float64)
    return np.moveaxis((codes * scale).reshape(v.shape), -1, axis)


WIDE = False


def mx_kscale(k):
    if not WIDE:
        return np.ones(k)
    levels = np.array([10, -10, 5, -5, 0])
    a = np.random.permutation(np.resize(levels, k // 512 * 4)).reshape(k // 512, 4)
    idx = np.arange(k)
    return np.exp2(a[idx // 512, idx % 128 // 32])


BF16 = ml_dtypes.bfloat16


def bf(x):
    return np.asarray(x, np.float32).astype(BF16)


def f64(x):
    return np.asarray(x).astype(np.float64)


B, N, G, L = 1024, 512, 128, 768
N2 = 2 * N
L2 = 2 * L
L_LIMIT = 1.0


def relu(v):
    return np.maximum(v, 0.0)


def setup_inputs():
    s, t = mx_kscale(N2), mx_kscale(L2)
    return {
        "Volt": bf(np.random.standard_normal((B, N2)) * s),
        "IM": bf(np.random.standard_normal((L2, N2)) / np.sqrt(N2) / s[None, :] * t[:, None]),
        "Ybr": bf(np.random.standard_normal((L2, L2)) / np.sqrt(L2) / t[None, :]),
        "n_o_mu_i_u": bf(np.random.standard_normal((B, L))),
    }


def reference(Volt, IM, Ybr, n_o_mu_i_u):
    mu = f64(n_o_mu_i_u)
    dv = mxq(f64(Volt), 1, "e4m3") @ mxq(f64(IM), 1, "e4m3").T
    Ibr = mxq(dv, 1, "e4m3") @ mxq(f64(Ybr), 1, "e4m3").T
    i_up = Ibr[:, :L] ** 2 + Ibr[:, L:] ** 2 - L_LIMIT ** 2
    out = np.sum(relu(i_up), axis=1)
    out = out + np.sum(np.abs(mu * i_up), axis=1)
    out = out + np.sum(relu(-mu), axis=1)
    return out

@@ -1,0 +1,287 @@
+from contextlib import ExitStack
+
+import concourse.mybir as mybir
+from concourse.masks import make_identity
+
+F32 = mybir.dt.float32
+BF16 = mybir.dt.bfloat16
+U32 = mybir.dt.uint32
+U8 = mybir.dt.uint8
+I32 = mybir.dt.int32
+FP8X4 = mybir.dt.float8_e4m3fn_x4
+ALU = mybir.AluOpType
+ACT = mybir.ActivationFunctionType
+AX = mybir.AxisListType
+
+P = 128
+B, N2, L2, L = 1024, 1024, 1536, 768
+JB = B // P
+FLOPS = 2 * B * N2 * L2 + 2 * B * L2 * L2
+PIN = False
+
+
+def tile_pinnlayer_pa_kernel(tc, Volt, IM, Ybr, n_o_mu_i_u, out):
+    nc = tc.nc
+    with ExitStack() as ctx:
+        if PIN:
+            ctx.enter_context(tc.manual_schedule())
+        keep = ctx.enter_context(tc.tile_pool(name="keep", bufs=1))
+        stage = ctx.enter_context(tc.tile_pool(name="stage", bufs=3))
+        epi = ctx.enter_context(tc.tile_pool(name="epi", bufs=2))
+        psum = ctx.enter_context(tc.psum_pool(name="psum", bufs=8))
+
+        ident = keep.tile([P, P], F32, name="ident")
+        make_identity(nc, ident[:])
+
+        volt_sb = keep.tile([P, JB, N2], BF16, name="volt_sb")
+        im_sb = keep.tile([P, 6, 2, N2], BF16, name="im_sb")
+        ybr_sb = keep.tile([P, 12, L2], BF16, name="ybr_sb")
+        mu_sb = keep.tile([P, JB, L], BF16, name="mu_sb")
+        a_sb = keep.tile([P, JB, L], BF16, name="a_sb")
+
+        vcodes = keep.tile([P, JB * 256], U32, name="vcodes", align_bytes=64)
+        vscales = keep.tile([P, JB * 256], U8, name="vscales", align_bytes=64)
+        icodes = keep.tile([P, 12 * 256], U32, name="icodes", align_bytes=64)
+        iscales = keep.tile([P, 12 * 256], U8, name="iscales", align_bytes=64)
+        ycodes = keep.tile([P, 3 * L2], U32, name="ycodes", align_bytes=64)
+        yscales = keep.tile([P, 3 * L2], U8, name="yscales", align_bytes=64)
+        dcodes = keep.tile([P, 3 * B], U32, name="dcodes", align_bytes=64)
+        dscales = keep.tile([P, 3 * B], U8, name="dscales", align_bytes=64)
+
+        ssq = keep.tile([P, JB, 4], F32, name="ssq")
+        sy = keep.tile([P, JB], F32, name="sy")
+        smin = keep.tile([P, JB], F32, name="smin")
+        srelu = keep.tile([P, JB, 8], F32, name="srelu")
+
+        volt_v = Volt.rearrange("(p j) k -> p j k", j=JB)
+        im_v = IM.rearrange("(t p e) k -> p t e k", t=6, e=2)
+        ybr_v = Ybr.rearrange("(r p) k -> p r k", p=P)
+        mu_v = n_o_mu_i_u.rearrange("(p j) l -> p j l", j=JB)
+
+        def load_im(t):
+            nc.sync.dma_start(out=im_sb[:, t, :, :], in_=im_v[:, t, :, :])
+
+        def load_volt(c):
+            nc.sync.dma_start(out=volt_sb[:, 2 * c:2 * c + 2, :], in_=volt_v[:, 2 * c:2 * c + 2, :])
+
+        def load_ybr(rp):
+            nc.sync.dma_start(out=ybr_sb[:, 2 * rp:2 * rp + 2, :], in_=ybr_v[:, 2 * rp:2 * rp + 2, :])
+
+        load_im(0)
+        load_im(1)
+        for c in range(4):
+            load_volt(c)
+        for t in range(2, 6):
+            load_im(t)
+        for rp in (0, 3, 1, 4, 2, 5):
+            load_ybr(rp)
+        for h in range(2):
+            nc.sync.dma_start(out=mu_sb[:, 4 * h:4 * h + 4, :], in_=mu_v[:, 4 * h:4 * h + 4, :])
+
+        volt_w = volt_sb[:].bitcast(F32)
+        im_w = im_sb[:].bitcast(F32)
+        ybr_w = ybr_sb[:].bitcast(F32)
+
+        load = {"v": 7000.0, "s": 0.0}
+        late = []
+        mark = {"done": 0}
+
+        def flush(upto):
+            for k in range(mark["done"], upto):
+                late[k]()
+            mark["done"] = max(mark["done"], upto)
+
+        def evac(dst, src):
+            if load["v"] < load["s"]:
+                nc.vector.tensor_copy(out=dst, in_=src)
+                load["v"] += 450.0
+            else:
+                nc.scalar.copy(out=dst, in_=src)
+                load["s"] += 450.0
+
+        def quantise(codes, scales, lo, words, src):
+            def go():
+                nc.vector.quantize_mx(
+                    out=codes[:, lo:lo + words].bitcast(FP8X4),
+                    scales=scales[:, lo:lo + words],
+                    in_=src,
+                )
+                load["v"] += 20.0 + 0.9 * words
+            late.append(go)
+            flush(len(late) - 1)
+
+        def transposes(srcs, codes, scales, lo):
+            grouped = stage.tile([P, 2, 1024], BF16, name="grouped", align_bytes=64)
+            gw = grouped[:].bitcast(F32)
+            for h in range(2):
+                bank = psum.tile([P, 512], F32, name="bank")
+                for q in range(4):
+                    nc.tensor.transpose(bank[:, 128 * q:128 * q + 128], srcs[h][q], ident[:])
+                evac(
+                    gw[:, h, :].rearrange("p (s r u) -> p s r u", s=2, u=2),
+                    bank[:].rearrange("p (s u r) -> p s r u", s=2, u=2),
+                )
+            quantise(codes, scales, lo, 512, grouped[:].rearrange("p h c -> p (h c)"))
+
+        def t_volt(c):
+            srcs = [[volt_w[:, 2 * c + h, 128 * q:128 * q + 128] for q in range(4)] for h in range(2)]
+            transposes(srcs, vcodes, vscales, 512 * c)
+
+        def t_im(t):
+            srcs = [[im_w[:, t, h, 128 * q:128 * q + 128] for q in range(4)] for h in range(2)]
+            transposes(srcs, icodes, iscales, 512 * t)
+
+        def t_ybr(c, g):
+            srcs = [
+                [ybr_w[:, 2 * rp + q // 2, 256 * g + 128 * (q % 2):256 * g + 128 * (q % 2) + 128] for q in range(4)]
+                for rp in (c, 3 + c)
+            ]
+            transposes(srcs, ycodes, yscales, L2 * g + 512 * c)
+
+        def stage1(g2, j0):
+            dgrp = stage.tile([P, 2, 512], BF16, name="dgrp", align_bytes=64)
+            for h in range(2):
+                j = j0 + h
+                bank = psum.tile([P, 512], F32, name="bank")
+                for t in range(4):
+                    for g in range(2):
+                        wi = 256 * (4 * g2 + t) + 128 * g
+                        wv = 256 * j + 128 * g
+                        nc.tensor.matmul_mx(
+                            out=bank[:, 128 * t:128 * t + 128],
+                            lhsT=icodes[:, wi:wi + 128].bitcast(FP8X4),
+                            lhsT_scale=iscales[:, wi:wi + 128],
+                            rhs=vcodes[:, wv:wv + 128].bitcast(FP8X4),
+                            rhs_scale=vscales[:, wv:wv + 128],
+                            start=(g == 0),
+                            stop=(g == 1),
+                        )
+                evac(
+                    dgrp[:, h, :].rearrange("p (b t) -> p b t", t=4),
+                    bank[:].rearrange("p (t b) -> p b t", t=4),
+                )
+            quantise(dcodes, dscales, B * g2 + 128 * j0, 256, dgrp[:].rearrange("p h c -> p (h c)"))
+
+        def mu_prep():
+            for h in range(2):
+                nc.vector.tensor_single_scalar(
+                    out=a_sb[:, 4 * h:4 * h + 4, :].bitcast(I32),
+                    in_=mu_sb[:, 4 * h:4 * h + 4, :].bitcast(I32),
+                    scalar=0x7FFF7FFF,
+                    op=ALU.bitwise_and,
+                )
+            for j in range(JB):
+                junk = epi.tile([P, L], F32, name="junk")
+                nc.vector.tensor_scalar(
+                    out=junk[:], in0=mu_sb[:, j, :], scalar1=0.0, scalar2=None,
+                    op0=ALU.min, op1=ALU.add, accum_out=smin[:, j:j + 1],
+                )
+
+        ys = {}
+
+        def stage2(j):
+            sq = epi.tile([P, 2, L], F32, name="sq", bufs=3)
+            for c in range(3):
+                bank = psum.tile([P, 512], F32, name="bank")
+                for g in range(3):
+                    wd = B * g + 128 * j
+                    wy = L2 * g + 512 * c
+                    nc.tensor.matmul_mx(
+                        out=bank[:],
+                        lhsT=dcodes[:, wd:wd + 128].bitcast(FP8X4),
+                        lhsT_scale=dscales[:, wd:wd + 128],
+                        rhs=ycodes[:, wy:wy + 512].bitcast(FP8X4),
+                        rhs_scale=yscales[:, wy:wy + 512],
+                        start=(g == 0),
+                        stop=(g == 2),
+                    )
+                nc.scalar.activation(
+                    out=sq[:, :, 256 * c:256 * c + 256],
+                    in_=bank[:].rearrange("p (a w) -> p a w", a=2),
+                    func=ACT.Square,
+                    accum_out=ssq[:, j, c:c + 1],
+                )
+                load["s"] += 470.0
+            x = epi.tile([P, L], F32, name="x")
+            nc.vector.scalar_tensor_tensor(
+                out=x[:], in0=sq[:, 0, :], scalar=-1.0, in1=sq[:, 1, :], op0=ALU.add, op1=ALU.add,
+            )
+            y = epi.tile([P, L], F32, name="y", bufs=3)
+            nc.vector.scalar_tensor_tensor(
+                out=y[:], in0=a_sb[:, j, :], scalar=0.5, in1=x[:], op0=ALU.add, op1=ALU.mult,
+                accum_out=sy[:, j:j + 1],
+            )
+            load["v"] += 1400.0
+            ys[j] = y
+
+        def relu_sum(j):
+            junk = epi.tile([P, L], F32, name="junk")
+            if load["v"] < load["s"]:
+                nc.vector.tensor_scalar(
+                    out=junk[:], in0=ys[j][:], scalar1=0.0, scalar2=None,
+                    op0=ALU.max, op1=ALU.add, accum_out=srelu[:, j, 0:1],
+                )
+                load["v"] += 700.0
+            else:
+                nc.scalar.activation(out=junk[:], in_=ys[j][:], func=ACT.Relu, accum_out=srelu[:, j, 0:1])
+                load["s"] += 700.0
+
+        t_im(0)
+        t_im(1)
+        t_volt(0)
+        t_volt(1)
+        t_volt(2)
+        t_volt(3)
+        flush(len(late))
+        stage1(0, 0)
+        stage1(0, 2)
+        t_im(2)
+        t_im(3)
+        stage1(0, 4)
+        stage1(0, 6)
+        t_im(4)
+        t_im(5)
+        t_ybr(0, 0)
+        flush(len(late))
+        stage1(1, 0)
+        stage1(1, 2)
+        t_ybr(0, 1)
+        t_ybr(0, 2)
+        t_ybr(1, 0)
+        stage1(1, 4)
+        stage1(1, 6)
+        t_ybr(1, 1)
+        t_ybr(1, 2)
+        t_ybr(2, 0)
+        flush(len(late))
+        stage1(2, 0)
+        stage1(2, 2)
+        t_ybr(2, 1)
+        t_ybr(2, 2)
+        stage1(2, 4)
+        stage1(2, 6)
+        flush(len(late))
+        mu_prep()
+        for j in range(JB):
+            stage2(j)
+            if j > 0:
+                relu_sum(j - 1)
+        relu_sum(JB - 1)
+
+        base = keep.tile([P, JB], F32, name="base")
+        nc.vector.tensor_scalar(
+            out=base[:], in0=smin[:], scalar1=-1.0, scalar2=-0.5 * L, op0=ALU.mult, op1=ALU.add,
+        )
+        t1 = keep.tile([P, JB], F32, name="t1")
+        nc.vector.tensor_reduce(out=t1[:], in_=ssq[:, :, 0:3], axis=AX.X, op=ALU.add)
+        t2 = keep.tile([P, JB], F32, name="t2")
+        nc.vector.scalar_tensor_tensor(
+            out=t2[:], in0=t1[:], scalar=0.5, in1=sy[:], op0=ALU.mult, op1=ALU.subtract,
+        )
+        t3 = keep.tile([P, JB], F32, name="t3")
+        nc.vector.scalar_tensor_tensor(
+            out=t3[:], in0=srelu[:, :, 0], scalar=2.0, in1=t2[:], op0=ALU.mult, op1=ALU.add,
+        )
+        res = keep.tile([P, JB], F32, name="res")
+        nc.vector.tensor_add(out=res[:], in0=t3[:], in1=base[:])
+        nc.sync.dma_start(out=out.rearrange("(p j) -> p j", j=JB), in_=res[:])

@@ -17,7 +17,21 @@ P = 128
 B, N2, L2, L = 1024, 1024, 1536, 768
 JB = B // P
 FLOPS = 2 * B * N2 * L2 + 2 * B * L2 * L2
-PIN = False
+PIN = True
+EV = "VSVVSSVSSVSSSSSVSVSSSSVSSSVSSVVSSSSVSVSSSSSSSVSSVSSSSSSVSSSSSV"
+ABS = "SVSVVSV"
+ABS_LAST = "SSS"
+SMIN = "SSVVSSVV"
+SEQ = (
+    ("I", 0), ("I", 1), ("V", 0), ("V", 1), ("V", 2), ("V", 3), ("F"), ("S", 0, 0),
+    ("S", 0, 2), ("I", 2), ("I", 3), ("S", 0, 4), ("S", 0, 6), ("I", 4), ("I", 5), ("Y", 0, 0),
+    ("F"), ("S", 1, 0), ("S", 1, 2), ("Y", 0, 1), ("Y", 0, 2), ("Y", 1, 0), ("S", 1, 4), ("S", 1, 6),
+    ("a", 0), ("Y", 1, 1), ("m", 2), ("Y", 1, 2), ("m", 1), ("Y", 2, 0), ("F"), ("a", 1),
+    ("S", 2, 0), ("S", 2, 2), ("Y", 2, 1), ("Y", 2, 2), ("S", 2, 4), ("m", 7), ("m", 5), ("m", 4),
+    ("S", 2, 6), ("m", 6), ("m", 3), ("F"), ("Z", 0), ("Z", 1), ("r", 1), ("m", 0),
+    ("Z", 2), ("Z", 3), ("r", 0), ("r", 3), ("Z", 4), ("r", 2), ("r", 4), ("Z", 5),
+    ("Z", 6), ("r", 5), ("Z", 7), ("r", 6),
+)
 
 
 def tile_pinnlayer_pa_kernel(tc, Volt, IM, Ybr, n_o_mu_i_u, out):
@@ -48,10 +62,17 @@ def tile_pinnlayer_pa_kernel(tc, Volt, IM, Ybr, n_o_mu_i_u, out):
         dcodes = keep.tile([P, 3 * B], U32, name="dcodes", align_bytes=64)
         dscales = keep.tile([P, 3 * B], U8, name="dscales", align_bytes=64)
 
-        ssq = keep.tile([P, JB, 4], F32, name="ssq")
-        sy = keep.tile([P, JB], F32, name="sy")
-        smin = keep.tile([P, JB], F32, name="smin")
-        srelu = keep.tile([P, JB, 8], F32, name="srelu")
+        acc_s = keep.tile([P, JB, 6], F32, name="acc_s")
+        acc_v = keep.tile([P, JB, 3], F32, name="acc_v")
+        negmu_s = keep.tile([P, JB], F32, name="negmu_s")
+        negmu_v = keep.tile([P, JB], F32, name="negmu_v")
+        warm = keep.tile([P, 1], F32, name="warm")
+        nc.vector.memset(warm[:], 0.0)
+        nc.vector.memset(acc_s[:], 0.0)
+        nc.vector.memset(acc_v[:], 0.0)
+        nc.vector.memset(negmu_s[:], 0.0)
+        nc.vector.memset(negmu_v[:], 0.0)
+        nc.scalar.activation(out=warm[:], in_=warm[:], func=ACT.Abs)
 
         volt_v = Volt.rearrange("(p j) k -> p j k", j=JB)
         im_v = IM.rearrange("(t p e) k -> p t e k", t=6, e=2)
@@ -82,9 +103,8 @@ def tile_pinnlayer_pa_kernel(tc, Volt, IM, Ybr, n_o_mu_i_u, out):
         im_w = im_sb[:].bitcast(F32)
         ybr_w = ybr_sb[:].bitcast(F32)
 
-        load = {"v": 7000.0, "s": 0.0}
         late = []
-        mark = {"done": 0}
+        mark = {"done": 0, "ev": 0}
 
         def flush(upto):
             for k in range(mark["done"], upto):
@@ -92,12 +112,12 @@ def tile_pinnlayer_pa_kernel(tc, Volt, IM, Ybr, n_o_mu_i_u, out):
             mark["done"] = max(mark["done"], upto)
 
         def evac(dst, src):
-            if load["v"] < load["s"]:
+            eng = EV[mark["ev"]]
+            mark["ev"] += 1
+            if eng == "V":
                 nc.vector.tensor_copy(out=dst, in_=src)
-                load["v"] += 450.0
             else:
                 nc.scalar.copy(out=dst, in_=src)
-                load["s"] += 450.0
 
         def quantise(codes, scales, lo, words, src):
             def go():
@@ -106,7 +126,6 @@ def tile_pinnlayer_pa_kernel(tc, Volt, IM, Ybr, n_o_mu_i_u, out):
                     scales=scales[:, lo:lo + words],
                     in_=src,
                 )
-                load["v"] += 20.0 + 0.9 * words
             late.append(go)
             flush(len(late) - 1)
 
@@ -162,25 +181,62 @@ def tile_pinnlayer_pa_kernel(tc, Volt, IM, Ybr, n_o_mu_i_u, out):
                 )
             quantise(dcodes, dscales, B * g2 + 128 * j0, 256, dgrp[:].rearrange("p h c -> p (h c)"))
 
-        def mu_prep():
-            for h in range(2):
-                nc.vector.tensor_single_scalar(
-                    out=a_sb[:, 4 * h:4 * h + 4, :].bitcast(I32),
-                    in_=mu_sb[:, 4 * h:4 * h + 4, :].bitcast(I32),
-                    scalar=0x7FFF7FFF,
-                    op=ALU.bitwise_and,
-                )
-            for j in range(JB):
-                junk = epi.tile([P, L], F32, name="junk")
+        def abs_mu(h):
+            nc.vector.tensor_single_scalar(
+                out=a_sb[:, 4 * h:4 * h + 4, :].bitcast(I32),
+                in_=mu_sb[:, 4 * h:4 * h + 4, :].bitcast(I32),
+                scalar=0x7FFF7FFF,
+                op=ALU.bitwise_and,
+            )
+
+        def sum_neg_mu(j):
+            if SMIN[j] == "V":
+                junk_v = epi.tile([P, L], F32, name="junk_v", bufs=1)
                 nc.vector.tensor_scalar(
-                    out=junk[:], in0=mu_sb[:, j, :], scalar1=0.0, scalar2=None,
-                    op0=ALU.min, op1=ALU.add, accum_out=smin[:, j:j + 1],
+                    out=junk_v[:], in0=mu_sb[:, j, :], scalar1=0.0, scalar2=None,
+                    op0=ALU.min, op1=ALU.add, accum_out=negmu_v[:, j:j + 1],
+                )
+            else:
+                junk_s = epi.tile([P, L], F32, name="junk_s", bufs=1)
+                nc.scalar.activation(
+                    out=junk_s[:], in_=mu_sb[:, j, :], func=ACT.Relu, scale=-1.0,
+                    accum_out=negmu_s[:, j:j + 1],
                 )
 
         ys = {}
 
+        def abs_sum(j, lo, hi, eng, col):
+            y = ys[j]
+            if eng == "V":
+                junk_v = epi.tile([P, L], F32, name="junk_v", bufs=1)
+                nc.vector.scalar_tensor_tensor(
+                    out=junk_v[:, lo:hi], in0=y[:, lo:hi], scalar=-1.0, in1=y[:, lo:hi],
+                    op0=ALU.mult, op1=ALU.max, accum_out=acc_v[:, j, col:col + 1],
+                )
+            else:
+                junk_s = epi.tile([P, L], F32, name="junk_s", bufs=1)
+                nc.scalar.activation(
+                    out=junk_s[:, lo:hi], in_=y[:, lo:hi], func=ACT.Abs, scale=2.0,
+                    accum_out=acc_s[:, j, 3 + col:4 + col],
+                )
+
+        def xy(j, sq, x, y, lo, hi):
+            nc.vector.scalar_tensor_tensor(
+                out=x[:, lo:hi], in0=sq[:, 0, lo:hi], scalar=-1.0, in1=sq[:, 1, lo:hi],
+                op0=ALU.add, op1=ALU.add,
+            )
+            nc.vector.scalar_tensor_tensor(
+                out=y[:, lo:hi], in0=a_sb[:, j, lo:hi], scalar=0.5, in1=x[:, lo:hi],
+                op0=ALU.add, op1=ALU.mult,
+            )
+
         def stage2(j):
+            flush(len(late))
+            last = j == JB - 1
             sq = epi.tile([P, 2, L], F32, name="sq", bufs=3)
+            x = epi.tile([P, L], F32, name="x")
+            y = epi.tile([P, L], F32, name="y", bufs=4)
+            ys[j] = y
             for c in range(3):
                 bank = psum.tile([P, 512], F32, name="bank")
                 for g in range(3):
@@ -199,89 +255,53 @@ def tile_pinnlayer_pa_kernel(tc, Volt, IM, Ybr, n_o_mu_i_u, out):
                     out=sq[:, :, 256 * c:256 * c + 256],
                     in_=bank[:].rearrange("p (a w) -> p a w", a=2),
                     func=ACT.Square,
-                    accum_out=ssq[:, j, c:c + 1],
+                    accum_out=acc_s[:, j, c:c + 1],
                 )
-                load["s"] += 470.0
-            x = epi.tile([P, L], F32, name="x")
-            nc.vector.scalar_tensor_tensor(
-                out=x[:], in0=sq[:, 0, :], scalar=-1.0, in1=sq[:, 1, :], op0=ALU.add, op1=ALU.add,
-            )
-            y = epi.tile([P, L], F32, name="y", bufs=3)
-            nc.vector.scalar_tensor_tensor(
-                out=y[:], in0=a_sb[:, j, :], scalar=0.5, in1=x[:], op0=ALU.add, op1=ALU.mult,
-                accum_out=sy[:, j:j + 1],
-            )
-            load["v"] += 1400.0
-            ys[j] = y
-
-        def relu_sum(j):
-            junk = epi.tile([P, L], F32, name="junk")
-            if load["v"] < load["s"]:
-                nc.vector.tensor_scalar(
-                    out=junk[:], in0=ys[j][:], scalar1=0.0, scalar2=None,
-                    op0=ALU.max, op1=ALU.add, accum_out=srelu[:, j, 0:1],
-                )
-                load["v"] += 700.0
+                if last:
+                    xy(j, sq, x, y, 256 * c, 256 * c + 256)
+                    if c > 0:
+                        abs_sum(j, 256 * (c - 1), 256 * c, ABS_LAST[c - 1], c - 1)
+            if last:
+                abs_sum(j, 512, 768, ABS_LAST[2], 2)
             else:
-                nc.scalar.activation(out=junk[:], in_=ys[j][:], func=ACT.Relu, accum_out=srelu[:, j, 0:1])
-                load["s"] += 700.0
+                xy(j, sq, x, y, 0, L)
 
-        t_im(0)
-        t_im(1)
-        t_volt(0)
-        t_volt(1)
-        t_volt(2)
-        t_volt(3)
-        flush(len(late))
-        stage1(0, 0)
-        stage1(0, 2)
-        t_im(2)
-        t_im(3)
-        stage1(0, 4)
-        stage1(0, 6)
-        t_im(4)
-        t_im(5)
-        t_ybr(0, 0)
-        flush(len(late))
-        stage1(1, 0)
-        stage1(1, 2)
-        t_ybr(0, 1)
-        t_ybr(0, 2)
-        t_ybr(1, 0)
-        stage1(1, 4)
-        stage1(1, 6)
-        t_ybr(1, 1)
-        t_ybr(1, 2)
-        t_ybr(2, 0)
-        flush(len(late))
-        stage1(2, 0)
-        stage1(2, 2)
-        t_ybr(2, 1)
-        t_ybr(2, 2)
-        stage1(2, 4)
-        stage1(2, 6)
-        flush(len(late))
-        mu_prep()
-        for j in range(JB):
-            stage2(j)
-            if j > 0:
-                relu_sum(j - 1)
-        relu_sum(JB - 1)
+        for tok in SEQ:
+            kind = tok[0]
+            args = tok[1:]
+            if kind == "I":
+                t_im(args[0])
+            elif kind == "V":
+                t_volt(args[0])
+            elif kind == "Y":
+                t_ybr(args[0], args[1])
+            elif kind == "S":
+                stage1(args[0], args[1])
+            elif kind == "F":
+                flush(len(late))
+            elif kind == "a":
+                abs_mu(args[0])
+            elif kind == "m":
+                sum_neg_mu(args[0])
+            elif kind == "Z":
+                stage2(args[0])
+            elif kind == "r":
+                abs_sum(args[0], 0, L, ABS[args[0]], 0)
 
         base = keep.tile([P, JB], F32, name="base")
         nc.vector.tensor_scalar(
-            out=base[:], in0=smin[:], scalar1=-1.0, scalar2=-0.5 * L, op0=ALU.mult, op1=ALU.add,
+            out=base[:], in0=negmu_v[:], scalar1=-1.0, scalar2=-0.5 * L, op0=ALU.mult, op1=ALU.add,
         )
-        t1 = keep.tile([P, JB], F32, name="t1")
-        nc.vector.tensor_reduce(out=t1[:], in_=ssq[:, :, 0:3], axis=AX.X, op=ALU.add)
-        t2 = keep.tile([P, JB], F32, name="t2")
-        nc.vector.scalar_tensor_tensor(
-            out=t2[:], in0=t1[:], scalar=0.5, in1=sy[:], op0=ALU.mult, op1=ALU.subtract,
-        )
-        t3 = keep.tile([P, JB], F32, name="t3")
-        nc.vector.scalar_tensor_tensor(
-            out=t3[:], in0=srelu[:, :, 0], scalar=2.0, in1=t2[:], op0=ALU.mult, op1=ALU.add,
-        )
+        base2 = keep.tile([P, JB], F32, name="base2")
+        nc.vector.tensor_add(out=base2[:], in0=base[:], in1=negmu_s[:])
+        rv = keep.tile([P, JB], F32, name="rv")
+        nc.vector.tensor_reduce(out=rv[:], in_=acc_v[:], axis=AX.X, op=ALU.add)
+        pre = keep.tile([P, JB], F32, name="pre")
+        nc.vector.tensor_add(out=pre[:], in0=rv[:], in1=base2[:])
+        rs = keep.tile([P, JB], F32, name="rs")
+        nc.vector.tensor_reduce(out=rs[:], in_=acc_s[:], axis=AX.X, op=ALU.add)
         res = keep.tile([P, JB], F32, name="res")
-        nc.vector.tensor_add(out=res[:], in0=t3[:], in1=base[:])
+        nc.vector.scalar_tensor_tensor(
+            out=res[:], in0=rs[:], scalar=0.5, in1=pre[:], op0=ALU.mult, op1=ALU.add,
+        )
         nc.sync.dma_start(out=out.rearrange("(p j) -> p j", j=JB), in_=res[:])

@@ -23,7 +23,8 @@ ABS = "SVSVVSV"
 ABS_LAST = "SSS"
 SMIN = "SSVVSSVV"
 SEQ = (
-    ("I", 0), ("I", 1), ("V", 0), ("V", 1), ("V", 2), ("V", 3), ("F"), ("S", 0, 0),
+    ("W"), ("W"), ("W"), ("W"), ("W"), ("W"),
+    ("I", 0), ("W"), ("I", 1), ("W"), ("V", 0), ("W"), ("V", 1), ("W"), ("V", 2), ("W"), ("V", 3), ("F"), ("S", 0, 0),
     ("S", 0, 2), ("I", 2), ("I", 3), ("S", 0, 4), ("S", 0, 6), ("I", 4), ("I", 5), ("Y", 0, 0),
     ("F"), ("S", 1, 0), ("S", 1, 2), ("Y", 0, 1), ("Y", 0, 2), ("Y", 1, 0), ("S", 1, 4), ("S", 1, 6),
     ("a", 0), ("Y", 1, 1), ("m", 2), ("Y", 1, 2), ("m", 1), ("Y", 2, 0), ("F"), ("a", 1),
@@ -68,6 +69,8 @@ def tile_pinnlayer_pa_kernel(tc, Volt, IM, Ybr, n_o_mu_i_u, out):
         negmu_v = keep.tile([P, JB], F32, name="negmu_v")
         warm = keep.tile([P, 1], F32, name="warm")
         nc.vector.memset(warm[:], 0.0)
+        zeros = keep.tile([P, 512], BF16, name="zeros")
+        nc.vector.memset(zeros[:], 0.0)
         nc.vector.memset(acc_s[:], 0.0)
         nc.vector.memset(acc_v[:], 0.0)
         nc.vector.memset(negmu_s[:], 0.0)
@@ -266,9 +269,16 @@ def tile_pinnlayer_pa_kernel(tc, Volt, IM, Ybr, n_o_mu_i_u, out):
             else:
                 xy(j, sq, x, y, 0, L)
 
+        idle_bank = psum.tile([P, 512], F32, name="bank")
+
+        def keep_warm():
+            nc.tensor.matmul(out=idle_bank[:], lhsT=zeros[:, 0:P], rhs=zeros[:], start=True, stop=True)
+
         for tok in SEQ:
             kind = tok[0]
             args = tok[1:]
+            if kind == "W":
+                keep_warm()
             if kind == "I":
                 t_im(args[0])
             elif kind == "V":

@@ -18,20 +18,19 @@ B, N2, L2, L = 1024, 1024, 1536, 768
 JB = B // P
 FLOPS = 2 * B * N2 * L2 + 2 * B * L2 * L2
 PIN = True
-EV = "VSVVSSVSSVSSSSSVSVSSSSVSSSVSSVVSSSSVSVSSSSSSSVSSVSSSSSSVSSSSSV"
-ABS = "SVSVVSV"
+EV = "SVSVVSSSSVVVSSSSSVSVSSSSSVVSSVSSSVSVSVSSSSVSSVSSVSSSSSSVSSSSVS"
+ABS = "SVSSSSV"
 ABS_LAST = "SSS"
-SMIN = "SSVVSSVV"
+SMIN = "SSVVVSVV"
 SEQ = (
-    ("W"), ("W"), ("W"), ("W"), ("W"), ("W"),
-    ("I", 0), ("W"), ("I", 1), ("W"), ("V", 0), ("W"), ("V", 1), ("W"), ("V", 2), ("W"), ("V", 3), ("F"), ("S", 0, 0),
-    ("S", 0, 2), ("I", 2), ("I", 3), ("S", 0, 4), ("S", 0, 6), ("I", 4), ("I", 5), ("Y", 0, 0),
-    ("F"), ("S", 1, 0), ("S", 1, 2), ("Y", 0, 1), ("Y", 0, 2), ("Y", 1, 0), ("S", 1, 4), ("S", 1, 6),
-    ("a", 0), ("Y", 1, 1), ("m", 2), ("Y", 1, 2), ("m", 1), ("Y", 2, 0), ("F"), ("a", 1),
-    ("S", 2, 0), ("S", 2, 2), ("Y", 2, 1), ("Y", 2, 2), ("S", 2, 4), ("m", 7), ("m", 5), ("m", 4),
-    ("S", 2, 6), ("m", 6), ("m", 3), ("F"), ("Z", 0), ("Z", 1), ("r", 1), ("m", 0),
-    ("Z", 2), ("Z", 3), ("r", 0), ("r", 3), ("Z", 4), ("r", 2), ("r", 4), ("Z", 5),
-    ("Z", 6), ("r", 5), ("Z", 7), ("r", 6),
+    ("I", 0), ("I", 1), ("V", 0), ("V", 1), ("V", 2), ("V", 3), ("F"), ("S", 0, 0),
+    ("S", 0, 2), ("I", 2), ("I", 3), ("S", 0, 4), ("S", 0, 6), ("m", 2), ("I", 4), ("I", 5),
+    ("m", 0), ("m", 1), ("F"), ("S", 1, 0), ("a", 0), ("S", 1, 2), ("Y", 0, 0), ("Y", 0, 1),
+    ("Y", 0, 2), ("S", 1, 4), ("S", 1, 6), ("Y", 1, 0), ("Y", 1, 1), ("Y", 1, 2), ("F"), ("S", 2, 0),
+    ("m", 3), ("S", 2, 2), ("Y", 2, 0), ("Y", 2, 1), ("Y", 2, 2), ("S", 2, 4), ("S", 2, 6), ("m", 4),
+    ("a", 1), ("F"), ("m", 5), ("Z", 0), ("Z", 1), ("r", 0), ("r", 1), ("Z", 2),
+    ("Z", 3), ("m", 6), ("r", 2), ("m", 7), ("Z", 4), ("r", 3), ("Z", 5), ("Z", 6),
+    ("r", 6), ("r", 5), ("r", 4), ("Z", 7),
 )
 
 
@@ -69,8 +68,6 @@ def tile_pinnlayer_pa_kernel(tc, Volt, IM, Ybr, n_o_mu_i_u, out):
         negmu_v = keep.tile([P, JB], F32, name="negmu_v")
         warm = keep.tile([P, 1], F32, name="warm")
         nc.vector.memset(warm[:], 0.0)
-        zeros = keep.tile([P, 512], BF16, name="zeros")
-        nc.vector.memset(zeros[:], 0.0)
         nc.vector.memset(acc_s[:], 0.0)
         nc.vector.memset(acc_v[:], 0.0)
         nc.vector.memset(negmu_s[:], 0.0)
@@ -97,10 +94,13 @@ def tile_pinnlayer_pa_kernel(tc, Volt, IM, Ybr, n_o_mu_i_u, out):
             load_volt(c)
         for t in range(2, 6):
             load_im(t)
+        def load_mu(h):
+            nc.sync.dma_start(out=mu_sb[:, 4 * h:4 * h + 4, :], in_=mu_v[:, 4 * h:4 * h + 4, :])
+
+        load_mu(0)
         for rp in (0, 3, 1, 4, 2, 5):
             load_ybr(rp)
-        for h in range(2):
-            nc.sync.dma_start(out=mu_sb[:, 4 * h:4 * h + 4, :], in_=mu_v[:, 4 * h:4 * h + 4, :])
+        load_mu(1)
 
         volt_w = volt_sb[:].bitcast(F32)
         im_w = im_sb[:].bitcast(F32)
@@ -269,16 +269,9 @@ def tile_pinnlayer_pa_kernel(tc, Volt, IM, Ybr, n_o_mu_i_u, out):
             else:
                 xy(j, sq, x, y, 0, L)
 
-        idle_bank = psum.tile([P, 512], F32, name="bank")
-
-        def keep_warm():
-            nc.tensor.matmul(out=idle_bank[:], lhsT=zeros[:, 0:P], rhs=zeros[:], start=True, stop=True)
-
         for tok in SEQ:
             kind = tok[0]
             args = tok[1:]
-            if kind == "W":
-                keep_warm()
             if kind == "I":
                 t_im(args[0])
             elif kind == "V":

@@ -18,19 +18,18 @@ B, N2, L2, L = 1024, 1024, 1536, 768
 JB = B // P
 FLOPS = 2 * B * N2 * L2 + 2 * B * L2 * L2
 PIN = True
-EV = "SVSVVSSSSVVVSSSSSVSVSSSSSVVSSVSSSVSVSVSSSSVSSVSSVSSSSSSVSSSSVS"
+EV = "SVSSVSSSVSSSSSVSVVSSVSSSSVSSSVSVSSSVSVSSSVVSSSSSVSSVSSSVSSSSVV"
 ABS = "SVSSSSV"
 ABS_LAST = "SSS"
-SMIN = "SSVVVSVV"
+SMIN = "SSVVSSVV"
 SEQ = (
-    ("I", 0), ("I", 1), ("V", 0), ("V", 1), ("V", 2), ("V", 3), ("F"), ("S", 0, 0),
-    ("S", 0, 2), ("I", 2), ("I", 3), ("S", 0, 4), ("S", 0, 6), ("m", 2), ("I", 4), ("I", 5),
-    ("m", 0), ("m", 1), ("F"), ("S", 1, 0), ("a", 0), ("S", 1, 2), ("Y", 0, 0), ("Y", 0, 1),
-    ("Y", 0, 2), ("S", 1, 4), ("S", 1, 6), ("Y", 1, 0), ("Y", 1, 1), ("Y", 1, 2), ("F"), ("S", 2, 0),
-    ("m", 3), ("S", 2, 2), ("Y", 2, 0), ("Y", 2, 1), ("Y", 2, 2), ("S", 2, 4), ("S", 2, 6), ("m", 4),
-    ("a", 1), ("F"), ("m", 5), ("Z", 0), ("Z", 1), ("r", 0), ("r", 1), ("Z", 2),
-    ("Z", 3), ("m", 6), ("r", 2), ("m", 7), ("Z", 4), ("r", 3), ("Z", 5), ("Z", 6),
-    ("r", 6), ("r", 5), ("r", 4), ("Z", 7),
+    ("I", 0), ("I", 1), ("V", 0), ("V", 1), ("V", 2), ("S", 0, 0), ("V", 3), ("S", 0, 2),
+    ("S", 0, 4), ("I", 2), ("I", 3), ("I", 4), ("m", 2), ("I", 5), ("S", 0, 6), ("m", 0),
+    ("a", 0), ("S", 1, 0), ("S", 1, 2), ("m", 1), ("S", 1, 4), ("S", 1, 6), ("Y", 0, 0), ("Y", 0, 1),
+    ("Y", 0, 2), ("Y", 1, 0), ("Y", 1, 1), ("S", 2, 0), ("S", 2, 2), ("Y", 1, 2), ("Y", 2, 0), ("Y", 2, 1),
+    ("Y", 2, 2), ("S", 2, 4), ("a", 1), ("m", 5), ("S", 2, 6), ("m", 4), ("m", 3), ("Z", 0),
+    ("Z", 1), ("r", 1), ("r", 0), ("Z", 2), ("m", 6), ("Z", 3), ("m", 7), ("r", 2),
+    ("Z", 4), ("r", 3), ("Z", 5), ("Z", 6), ("r", 4), ("r", 6), ("r", 5), ("Z", 7),
 )
 
 
@@ -122,17 +121,20 @@ def tile_pinnlayer_pa_kernel(tc, Volt, IM, Ybr, n_o_mu_i_u, out):
             else:
                 nc.scalar.copy(out=dst, in_=src)
 
-        def quantise(codes, scales, lo, words, src):
+        written = set()
+
+        def quantise(codes, scales, lo, words, src, key):
             def go():
                 nc.vector.quantize_mx(
                     out=codes[:, lo:lo + words].bitcast(FP8X4),
                     scales=scales[:, lo:lo + words],
                     in_=src,
                 )
+                written.add(key)
             late.append(go)
             flush(len(late) - 1)
 
-        def transposes(srcs, codes, scales, lo):
+        def transposes(srcs, codes, scales, lo, key):
             grouped = stage.tile([P, 2, 1024], BF16, name="grouped", align_bytes=64)
             gw = grouped[:].bitcast(F32)
             for h in range(2):
@@ -143,24 +145,26 @@ def tile_pinnlayer_pa_kernel(tc, Volt, IM, Ybr, n_o_mu_i_u, out):
                     gw[:, h, :].rearrange("p (s r u) -> p s r u", s=2, u=2),
                     bank[:].rearrange("p (s u r) -> p s r u", s=2, u=2),
                 )
-            quantise(codes, scales, lo, 512, grouped[:].rearrange("p h c -> p (h c)"))
+            quantise(codes, scales, lo, 512, grouped[:].rearrange("p h c -> p (h c)"), key)
 
         def t_volt(c):
             srcs = [[volt_w[:, 2 * c + h, 128 * q:128 * q + 128] for q in range(4)] for h in range(2)]
-            transposes(srcs, vcodes, vscales, 512 * c)
+            transposes(srcs, vcodes, vscales, 512 * c, ("V", c))
 
         def t_im(t):
             srcs = [[im_w[:, t, h, 128 * q:128 * q + 128] for q in range(4)] for h in range(2)]
-            transposes(srcs, icodes, iscales, 512 * t)
+            transposes(srcs, icodes, iscales, 512 * t, ("I", t))
 
         def t_ybr(c, g):
             srcs = [
                 [ybr_w[:, 2 * rp + q // 2, 256 * g + 128 * (q % 2):256 * g + 128 * (q % 2) + 128] for q in range(4)]
                 for rp in (c, 3 + c)
             ]
-            transposes(srcs, ycodes, yscales, L2 * g + 512 * c)
+            transposes(srcs, ycodes, yscales, L2 * g + 512 * c, ("Y", c, g))
 
         def stage1(g2, j0):
+            if not all(k in written for k in (("I", 2 * g2), ("I", 2 * g2 + 1), ("V", j0 // 2))):
+                flush(len(late))
             dgrp = stage.tile([P, 2, 512], BF16, name="dgrp", align_bytes=64)
             for h in range(2):
                 j = j0 + h
@@ -182,7 +186,7 @@ def tile_pinnlayer_pa_kernel(tc, Volt, IM, Ybr, n_o_mu_i_u, out):
                     dgrp[:, h, :].rearrange("p (b t) -> p b t", t=4),
                     bank[:].rearrange("p (t b) -> p b t", t=4),
                 )
-            quantise(dcodes, dscales, B * g2 + 128 * j0, 256, dgrp[:].rearrange("p h c -> p (h c)"))
+            quantise(dcodes, dscales, B * g2 + 128 * j0, 256, dgrp[:].rearrange("p h c -> p (h c)"), ("D", g2, j0))
 
         def abs_mu(h):
             nc.vector.tensor_single_scalar(

@@ -18,18 +18,19 @@ B, N2, L2, L = 1024, 1024, 1536, 768
 JB = B // P
 FLOPS = 2 * B * N2 * L2 + 2 * B * L2 * L2
 PIN = True
-EV = "SVSSVSSSVSSSSSVSVVSSVSSSSVSSSVSVSSSVSVSSSVVSSSSSVSSVSSSVSSSSVV"
+EV = "VVSSVSSSSSVSSSVVSSSVSSSSVSVSSSSSSVSVVVSSVSVSSVSSSSSVSSSVSSSSVV"
 ABS = "SVSSSSV"
 ABS_LAST = "SSS"
-SMIN = "SSVVSSVV"
+SMIN = "VSSVSSVV"
 SEQ = (
-    ("I", 0), ("I", 1), ("V", 0), ("V", 1), ("V", 2), ("S", 0, 0), ("V", 3), ("S", 0, 2),
-    ("S", 0, 4), ("I", 2), ("I", 3), ("I", 4), ("m", 2), ("I", 5), ("S", 0, 6), ("m", 0),
-    ("a", 0), ("S", 1, 0), ("S", 1, 2), ("m", 1), ("S", 1, 4), ("S", 1, 6), ("Y", 0, 0), ("Y", 0, 1),
-    ("Y", 0, 2), ("Y", 1, 0), ("Y", 1, 1), ("S", 2, 0), ("S", 2, 2), ("Y", 1, 2), ("Y", 2, 0), ("Y", 2, 1),
-    ("Y", 2, 2), ("S", 2, 4), ("a", 1), ("m", 5), ("S", 2, 6), ("m", 4), ("m", 3), ("Z", 0),
-    ("Z", 1), ("r", 1), ("r", 0), ("Z", 2), ("m", 6), ("Z", 3), ("m", 7), ("r", 2),
-    ("Z", 4), ("r", 3), ("Z", 5), ("Z", 6), ("r", 4), ("r", 6), ("r", 5), ("Z", 7),
+    ("I", 0), ("I", 1), ("V", 0), ("V", 1), ("V", 2), ("S", 0, 0), ("S", 0, 2), ("S", 0, 4),
+    ("V", 3), ("I", 2), ("I", 3), ("I", 4), ("I", 5), ("S", 0, 6), ("a", 0), ("m", 1),
+    ("m", 0), ("S", 1, 0), ("S", 1, 2), ("S", 1, 4), ("S", 1, 6), ("m", 2), ("S", 2, 0), ("S", 2, 2),
+    ("Y", 0, 0), ("Y", 0, 1), ("Y", 0, 2), ("Y", 1, 0), ("Y", 1, 1), ("Y", 1, 2), ("S", 2, 4), ("S", 2, 6),
+    ("Y", 2, 0), ("Y", 2, 1), ("Y", 2, 2), ("z", 0, 0), ("z", 1, 0), ("m", 4), ("a", 1), ("z", 1, 1),
+    ("m", 3), ("z", 0, 1), ("m", 7), ("z", 0, 2), ("m", 5), ("z", 1, 2), ("Z", 2), ("r", 0),
+    ("Z", 3), ("m", 6), ("r", 1), ("r", 2), ("Z", 4), ("r", 3), ("Z", 5), ("Z", 6),
+    ("r", 5), ("r", 4), ("r", 6), ("Z", 7),
 )
 
 
@@ -237,41 +238,49 @@ def tile_pinnlayer_pa_kernel(tc, Volt, IM, Ybr, n_o_mu_i_u, out):
                 op0=ALU.add, op1=ALU.mult,
             )
 
-        def stage2(j):
+        open_tiles = {}
+
+        def stage2_bank(j, c):
             flush(len(late))
             last = j == JB - 1
-            sq = epi.tile([P, 2, L], F32, name="sq", bufs=3)
-            x = epi.tile([P, L], F32, name="x")
-            y = epi.tile([P, L], F32, name="y", bufs=4)
-            ys[j] = y
-            for c in range(3):
-                bank = psum.tile([P, 512], F32, name="bank")
-                for g in range(3):
-                    wd = B * g + 128 * j
-                    wy = L2 * g + 512 * c
-                    nc.tensor.matmul_mx(
-                        out=bank[:],
-                        lhsT=dcodes[:, wd:wd + 128].bitcast(FP8X4),
-                        lhsT_scale=dscales[:, wd:wd + 128],
-                        rhs=ycodes[:, wy:wy + 512].bitcast(FP8X4),
-                        rhs_scale=yscales[:, wy:wy + 512],
-                        start=(g == 0),
-                        stop=(g == 2),
-                    )
-                nc.scalar.activation(
-                    out=sq[:, :, 256 * c:256 * c + 256],
-                    in_=bank[:].rearrange("p (a w) -> p a w", a=2),
-                    func=ACT.Square,
-                    accum_out=acc_s[:, j, c:c + 1],
+            if j not in open_tiles:
+                sq = epi.tile([P, 2, L], F32, name="sq", bufs=3)
+                x = epi.tile([P, L], F32, name="x")
+                y = epi.tile([P, L], F32, name="y", bufs=4)
+                open_tiles[j] = (sq, x, y)
+                ys[j] = y
+            sq, x, y = open_tiles[j]
+            bank = psum.tile([P, 512], F32, name="bank")
+            for g in range(3):
+                wd = B * g + 128 * j
+                wy = L2 * g + 512 * c
+                nc.tensor.matmul_mx(
+                    out=bank[:],
+                    lhsT=dcodes[:, wd:wd + 128].bitcast(FP8X4),
+                    lhsT_scale=dscales[:, wd:wd + 128],
+                    rhs=ycodes[:, wy:wy + 512].bitcast(FP8X4),
+                    rhs_scale=yscales[:, wy:wy + 512],
+                    start=(g == 0),
+                    stop=(g == 2),
                 )
-                if last:
-                    xy(j, sq, x, y, 256 * c, 256 * c + 256)
-                    if c > 0:
-                        abs_sum(j, 256 * (c - 1), 256 * c, ABS_LAST[c - 1], c - 1)
+            nc.scalar.activation(
+                out=sq[:, :, 256 * c:256 * c + 256],
+                in_=bank[:].rearrange("p (a w) -> p a w", a=2),
+                func=ACT.Square,
+                accum_out=acc_s[:, j, c:c + 1],
+            )
             if last:
-                abs_sum(j, 512, 768, ABS_LAST[2], 2)
-            else:
+                xy(j, sq, x, y, 256 * c, 256 * c + 256)
+                if c > 0:
+                    abs_sum(j, 256 * (c - 1), 256 * c, ABS_LAST[c - 1], c - 1)
+                if c == 2:
+                    abs_sum(j, 512, 768, ABS_LAST[2], 2)
+            elif c == 2:
                 xy(j, sq, x, y, 0, L)
+
+        def stage2(j):
+            for c in range(3):
+                stage2_bank(j, c)
 
         for tok in SEQ:
             kind = tok[0]
@@ -292,6 +301,8 @@ def tile_pinnlayer_pa_kernel(tc, Volt, IM, Ybr, n_o_mu_i_u, out):
                 sum_neg_mu(args[0])
             elif kind == "Z":
                 stage2(args[0])
+            elif kind == "z":
+                stage2_bank(args[0], args[1])
             elif kind == "r":
                 abs_sum(args[0], 0, L, ABS[args[0]], 0)
 

@@ -18,19 +18,19 @@ B, N2, L2, L = 1024, 1024, 1536, 768
 JB = B // P
 FLOPS = 2 * B * N2 * L2 + 2 * B * L2 * L2
 PIN = True
-EV = "VVSSVSSSSSVSSSVVSSSVSSSSVSVSSSSSSVSVVVSSVSVSSVSSSSSVSSSVSSSSVV"
+EV = "SVSVVSSSSVVVSSSSSVSVSSSSSVVSSVSSSVSVSVSSSSVSSVSSVSSSSSSVSSSSVS"
 ABS = "SVSSSSV"
 ABS_LAST = "SSS"
-SMIN = "VSSVSSVV"
+SMIN = "SSVVVSVV"
 SEQ = (
-    ("I", 0), ("I", 1), ("V", 0), ("V", 1), ("V", 2), ("S", 0, 0), ("S", 0, 2), ("S", 0, 4),
-    ("V", 3), ("I", 2), ("I", 3), ("I", 4), ("I", 5), ("S", 0, 6), ("a", 0), ("m", 1),
-    ("m", 0), ("S", 1, 0), ("S", 1, 2), ("S", 1, 4), ("S", 1, 6), ("m", 2), ("S", 2, 0), ("S", 2, 2),
-    ("Y", 0, 0), ("Y", 0, 1), ("Y", 0, 2), ("Y", 1, 0), ("Y", 1, 1), ("Y", 1, 2), ("S", 2, 4), ("S", 2, 6),
-    ("Y", 2, 0), ("Y", 2, 1), ("Y", 2, 2), ("z", 0, 0), ("z", 1, 0), ("m", 4), ("a", 1), ("z", 1, 1),
-    ("m", 3), ("z", 0, 1), ("m", 7), ("z", 0, 2), ("m", 5), ("z", 1, 2), ("Z", 2), ("r", 0),
-    ("Z", 3), ("m", 6), ("r", 1), ("r", 2), ("Z", 4), ("r", 3), ("Z", 5), ("Z", 6),
-    ("r", 5), ("r", 4), ("r", 6), ("Z", 7),
+    ("I", 0), ("I", 1), ("V", 0), ("V", 1), ("V", 2), ("V", 3), ("F"), ("S", 0, 0),
+    ("S", 0, 2), ("I", 2), ("I", 3), ("S", 0, 4), ("S", 0, 6), ("m", 2), ("I", 4), ("I", 5),
+    ("m", 0), ("m", 1), ("F"), ("S", 1, 0), ("a", 0), ("S", 1, 2), ("Y", 0, 0), ("Y", 0, 1),
+    ("Y", 0, 2), ("S", 1, 4), ("S", 1, 6), ("Y", 1, 0), ("Y", 1, 1), ("Y", 1, 2), ("F"), ("S", 2, 0),
+    ("m", 3), ("S", 2, 2), ("Y", 2, 0), ("Y", 2, 1), ("Y", 2, 2), ("S", 2, 4), ("S", 2, 6), ("m", 4),
+    ("a", 1), ("F"), ("m", 5), ("Z", 0), ("Z", 1), ("r", 0), ("r", 1), ("Z", 2),
+    ("Z", 3), ("m", 6), ("r", 2), ("m", 7), ("Z", 4), ("r", 3), ("Z", 5), ("Z", 6),
+    ("r", 6), ("r", 5), ("r", 4), ("Z", 7),
 )
 
 
@@ -122,20 +122,17 @@ def tile_pinnlayer_pa_kernel(tc, Volt, IM, Ybr, n_o_mu_i_u, out):
             else:
                 nc.scalar.copy(out=dst, in_=src)
 
-        written = set()
-
-        def quantise(codes, scales, lo, words, src, key):
+        def quantise(codes, scales, lo, words, src):
             def go():
                 nc.vector.quantize_mx(
                     out=codes[:, lo:lo + words].bitcast(FP8X4),
                     scales=scales[:, lo:lo + words],
                     in_=src,
                 )
-                written.add(key)
             late.append(go)
             flush(len(late) - 1)
 
-        def transposes(srcs, codes, scales, lo, key):
+        def transposes(srcs, codes, scales, lo):
             grouped = stage.tile([P, 2, 1024], BF16, name="grouped", align_bytes=64)
             gw = grouped[:].bitcast(F32)
             for h in range(2):
@@ -146,26 +143,24 @@ def tile_pinnlayer_pa_kernel(tc, Volt, IM, Ybr, n_o_mu_i_u, out):
                     gw[:, h, :].rearrange("p (s r u) -> p s r u", s=2, u=2),
                     bank[:].rearrange("p (s u r) -> p s r u", s=2, u=2),
                 )
-            quantise(codes, scales, lo, 512, grouped[:].rearrange("p h c -> p (h c)"), key)
+            quantise(codes, scales, lo, 512, grouped[:].rearrange("p h c -> p (h c)"))
 
         def t_volt(c):
             srcs = [[volt_w[:, 2 * c + h, 128 * q:128 * q + 128] for q in range(4)] for h in range(2)]
-            transposes(srcs, vcodes, vscales, 512 * c, ("V", c))
+            transposes(srcs, vcodes, vscales, 512 * c)
 
         def t_im(t):
             srcs = [[im_w[:, t, h, 128 * q:128 * q + 128] for q in range(4)] for h in range(2)]
-            transposes(srcs, icodes, iscales, 512 * t, ("I", t))
+            transposes(srcs, icodes, iscales, 512 * t)
 
         def t_ybr(c, g):
             srcs = [
                 [ybr_w[:, 2 * rp + q // 2, 256 * g + 128 * (q % 2):256 * g + 128 * (q % 2) + 128] for q in range(4)]
                 for rp in (c, 3 + c)
             ]
-            transposes(srcs, ycodes, yscales, L2 * g + 512 * c, ("Y", c, g))
+            transposes(srcs, ycodes, yscales, L2 * g + 512 * c)
 
         def stage1(g2, j0):
-            if not all(k in written for k in (("I", 2 * g2), ("I", 2 * g2 + 1), ("V", j0 // 2))):
-                flush(len(late))
             dgrp = stage.tile([P, 2, 512], BF16, name="dgrp", align_bytes=64)
             for h in range(2):
                 j = j0 + h
@@ -187,7 +182,7 @@ def tile_pinnlayer_pa_kernel(tc, Volt, IM, Ybr, n_o_mu_i_u, out):
                     dgrp[:, h, :].rearrange("p (b t) -> p b t", t=4),
                     bank[:].rearrange("p (t b) -> p b t", t=4),
                 )
-            quantise(dcodes, dscales, B * g2 + 128 * j0, 256, dgrp[:].rearrange("p h c -> p (h c)"), ("D", g2, j0))
+            quantise(dcodes, dscales, B * g2 + 128 * j0, 256, dgrp[:].rearrange("p h c -> p (h c)"))
 
         def abs_mu(h):
             nc.vector.tensor_single_scalar(
@@ -199,9 +194,9 @@ def tile_pinnlayer_pa_kernel(tc, Volt, IM, Ybr, n_o_mu_i_u, out):
 
         def sum_neg_mu(j):
             if SMIN[j] == "V":
-                junk_v = epi.tile([P, L], F32, name="junk_v", bufs=1)
+                junk_b = epi.tile([P, L], BF16, name="junk_b", bufs=1)
                 nc.vector.tensor_scalar(
-                    out=junk_v[:], in0=mu_sb[:, j, :], scalar1=0.0, scalar2=None,
+                    out=junk_b[:], in0=mu_sb[:, j, :], scalar1=0.0, scalar2=None,
                     op0=ALU.min, op1=ALU.add, accum_out=negmu_v[:, j:j + 1],
                 )
             else:
@@ -238,49 +233,41 @@ def tile_pinnlayer_pa_kernel(tc, Volt, IM, Ybr, n_o_mu_i_u, out):
                 op0=ALU.add, op1=ALU.mult,
             )
 
-        open_tiles = {}
-
-        def stage2_bank(j, c):
+        def stage2(j):
             flush(len(late))
             last = j == JB - 1
-            if j not in open_tiles:
-                sq = epi.tile([P, 2, L], F32, name="sq", bufs=3)
-                x = epi.tile([P, L], F32, name="x")
-                y = epi.tile([P, L], F32, name="y", bufs=4)
-                open_tiles[j] = (sq, x, y)
-                ys[j] = y
-            sq, x, y = open_tiles[j]
-            bank = psum.tile([P, 512], F32, name="bank")
-            for g in range(3):
-                wd = B * g + 128 * j
-                wy = L2 * g + 512 * c
-                nc.tensor.matmul_mx(
-                    out=bank[:],
-                    lhsT=dcodes[:, wd:wd + 128].bitcast(FP8X4),
-                    lhsT_scale=dscales[:, wd:wd + 128],
-                    rhs=ycodes[:, wy:wy + 512].bitcast(FP8X4),
-                    rhs_scale=yscales[:, wy:wy + 512],
-                    start=(g == 0),
-                    stop=(g == 2),
-                )
-            nc.scalar.activation(
-                out=sq[:, :, 256 * c:256 * c + 256],
-                in_=bank[:].rearrange("p (a w) -> p a w", a=2),
-                func=ACT.Square,
-                accum_out=acc_s[:, j, c:c + 1],
-            )
-            if last:
-                xy(j, sq, x, y, 256 * c, 256 * c + 256)
-                if c > 0:
-                    abs_sum(j, 256 * (c - 1), 256 * c, ABS_LAST[c - 1], c - 1)
-                if c == 2:
-                    abs_sum(j, 512, 768, ABS_LAST[2], 2)
-            elif c == 2:
-                xy(j, sq, x, y, 0, L)
-
-        def stage2(j):
+            sq = epi.tile([P, 2, L], F32, name="sq", bufs=3)
+            x = epi.tile([P, L], F32, name="x")
+            y = epi.tile([P, L], F32, name="y", bufs=4)
+            ys[j] = y
             for c in range(3):
-                stage2_bank(j, c)
+                bank = psum.tile([P, 512], F32, name="bank")
+                for g in range(3):
+                    wd = B * g + 128 * j
+                    wy = L2 * g + 512 * c
+                    nc.tensor.matmul_mx(
+                        out=bank[:],
+                        lhsT=dcodes[:, wd:wd + 128].bitcast(FP8X4),
+                        lhsT_scale=dscales[:, wd:wd + 128],
+                        rhs=ycodes[:, wy:wy + 512].bitcast(FP8X4),
+                        rhs_scale=yscales[:, wy:wy + 512],
+                        start=(g == 0),
+                        stop=(g == 2),
+                    )
+                nc.scalar.activation(
+                    out=sq[:, :, 256 * c:256 * c + 256],
+                    in_=bank[:].rearrange("p (a w) -> p a w", a=2),
+                    func=ACT.Square,
+                    accum_out=acc_s[:, j, c:c + 1],
+                )
+                if last:
+                    xy(j, sq, x, y, 256 * c, 256 * c + 256)
+                    if c > 0:
+                        abs_sum(j, 256 * (c - 1), 256 * c, ABS_LAST[c - 1], c - 1)
+            if last:
+                abs_sum(j, 512, 768, ABS_LAST[2], 2)
+            else:
+                xy(j, sq, x, y, 0, L)
 
         for tok in SEQ:
             kind = tok[0]
@@ -301,8 +288,6 @@ def tile_pinnlayer_pa_kernel(tc, Volt, IM, Ybr, n_o_mu_i_u, out):
                 sum_neg_mu(args[0])
             elif kind == "Z":
                 stage2(args[0])
-            elif kind == "z":
-                stage2_bank(args[0], args[1])
             elif kind == "r":
                 abs_sum(args[0], 0, L, ABS[args[0]], 0)
 

@@ -18,19 +18,17 @@ B, N2, L2, L = 1024, 1024, 1536, 768
 JB = B // P
 FLOPS = 2 * B * N2 * L2 + 2 * B * L2 * L2
 PIN = True
-EV = "SVSVVSSSSVVVSSSSSVSVSSSSSVVSSVSSSVSVSVSSSSVSSVSSVSSSSSSVSSSSVS"
+EV = "SVVSVSSVSSVSSVSSSVSVSSSSSVSSSVSSSVSSSVSSSSVSSVSSVSSSSSSVSSSSVS"
 ABS = "SVSSSSV"
 ABS_LAST = "SSS"
-SMIN = "SSVVVSVV"
 SEQ = (
-    ("I", 0), ("I", 1), ("V", 0), ("V", 1), ("V", 2), ("V", 3), ("F"), ("S", 0, 0),
-    ("S", 0, 2), ("I", 2), ("I", 3), ("S", 0, 4), ("S", 0, 6), ("m", 2), ("I", 4), ("I", 5),
-    ("m", 0), ("m", 1), ("F"), ("S", 1, 0), ("a", 0), ("S", 1, 2), ("Y", 0, 0), ("Y", 0, 1),
-    ("Y", 0, 2), ("S", 1, 4), ("S", 1, 6), ("Y", 1, 0), ("Y", 1, 1), ("Y", 1, 2), ("F"), ("S", 2, 0),
-    ("m", 3), ("S", 2, 2), ("Y", 2, 0), ("Y", 2, 1), ("Y", 2, 2), ("S", 2, 4), ("S", 2, 6), ("m", 4),
-    ("a", 1), ("F"), ("m", 5), ("Z", 0), ("Z", 1), ("r", 0), ("r", 1), ("Z", 2),
-    ("Z", 3), ("m", 6), ("r", 2), ("m", 7), ("Z", 4), ("r", 3), ("Z", 5), ("Z", 6),
-    ("r", 6), ("r", 5), ("r", 4), ("Z", 7),
+    ("I", 0), ("I", 1), ("V", 0), ("V", 1), ("V", 2), ("V", 3), ("S", 0, 0), ("S", 0, 2),
+    ("I", 2), ("I", 3), ("S", 0, 4), ("S", 0, 6), ("m", 2), ("a", 0), ("I", 4), ("I", 5),
+    ("S", 1, 0), ("S", 1, 2), ("m", 0), ("Y", 0, 0), ("Y", 0, 1), ("Y", 0, 2), ("S", 1, 4), ("S", 1, 6),
+    ("Y", 1, 0), ("m", 1), ("Y", 1, 1), ("Y", 1, 2), ("S", 2, 0), ("S", 2, 2), ("Y", 2, 0), ("Y", 2, 1),
+    ("Y", 2, 2), ("S", 2, 4), ("m", 3), ("a", 1), ("m", 7), ("S", 2, 6), ("m", 4), ("m", 5),
+    ("Z", 0), ("Z", 1), ("Z", 2), ("r", 0), ("r", 1), ("Z", 3), ("r", 2), ("Z", 4),
+    ("Z", 5), ("Z", 6), ("m", 6), ("r", 4), ("r", 5), ("r", 3), ("r", 6), ("Z", 7),
 )
 
 
@@ -64,14 +62,11 @@ def tile_pinnlayer_pa_kernel(tc, Volt, IM, Ybr, n_o_mu_i_u, out):
 
         acc_s = keep.tile([P, JB, 6], F32, name="acc_s")
         acc_v = keep.tile([P, JB, 3], F32, name="acc_v")
-        negmu_s = keep.tile([P, JB], F32, name="negmu_s")
         negmu_v = keep.tile([P, JB], F32, name="negmu_v")
         warm = keep.tile([P, 1], F32, name="warm")
         nc.vector.memset(warm[:], 0.0)
         nc.vector.memset(acc_s[:], 0.0)
         nc.vector.memset(acc_v[:], 0.0)
-        nc.vector.memset(negmu_s[:], 0.0)
-        nc.vector.memset(negmu_v[:], 0.0)
         nc.scalar.activation(out=warm[:], in_=warm[:], func=ACT.Abs)
 
         volt_v = Volt.rearrange("(p j) k -> p j k", j=JB)
@@ -122,17 +117,20 @@ def tile_pinnlayer_pa_kernel(tc, Volt, IM, Ybr, n_o_mu_i_u, out):
             else:
                 nc.scalar.copy(out=dst, in_=src)
 
-        def quantise(codes, scales, lo, words, src):
+        written = set()
+
+        def quantise(codes, scales, lo, words, src, key):
             def go():
                 nc.vector.quantize_mx(
                     out=codes[:, lo:lo + words].bitcast(FP8X4),
                     scales=scales[:, lo:lo + words],
                     in_=src,
                 )
+                written.add(key)
             late.append(go)
             flush(len(late) - 1)
 
-        def transposes(srcs, codes, scales, lo):
+        def transposes(srcs, codes, scales, lo, key):
             grouped = stage.tile([P, 2, 1024], BF16, name="grouped", align_bytes=64)
             gw = grouped[:].bitcast(F32)
             for h in range(2):
@@ -143,24 +141,26 @@ def tile_pinnlayer_pa_kernel(tc, Volt, IM, Ybr, n_o_mu_i_u, out):
                     gw[:, h, :].rearrange("p (s r u) -> p s r u", s=2, u=2),
                     bank[:].rearrange("p (s u r) -> p s r u", s=2, u=2),
                 )
-            quantise(codes, scales, lo, 512, grouped[:].rearrange("p h c -> p (h c)"))
+            quantise(codes, scales, lo, 512, grouped[:].rearrange("p h c -> p (h c)"), key)
 
         def t_volt(c):
             srcs = [[volt_w[:, 2 * c + h, 128 * q:128 * q + 128] for q in range(4)] for h in range(2)]
-            transposes(srcs, vcodes, vscales, 512 * c)
+            transposes(srcs, vcodes, vscales, 512 * c, ("V", c))
 
         def t_im(t):
             srcs = [[im_w[:, t, h, 128 * q:128 * q + 128] for q in range(4)] for h in range(2)]
-            transposes(srcs, icodes, iscales, 512 * t)
+            transposes(srcs, icodes, iscales, 512 * t, ("I", t))
 
         def t_ybr(c, g):
             srcs = [
                 [ybr_w[:, 2 * rp + q // 2, 256 * g + 128 * (q % 2):256 * g + 128 * (q % 2) + 128] for q in range(4)]
                 for rp in (c, 3 + c)
             ]
-            transposes(srcs, ycodes, yscales, L2 * g + 512 * c)
+            transposes(srcs, ycodes, yscales, L2 * g + 512 * c, ("Y", c, g))
 
         def stage1(g2, j0):
+            if not all(k in written for k in (("I", 2 * g2), ("I", 2 * g2 + 1), ("V", j0 // 2))):
+                flush(len(late))
             dgrp = stage.tile([P, 2, 512], BF16, name="dgrp", align_bytes=64)
             for h in range(2):
                 j = j0 + h
@@ -182,7 +182,7 @@ def tile_pinnlayer_pa_kernel(tc, Volt, IM, Ybr, n_o_mu_i_u, out):
                     dgrp[:, h, :].rearrange("p (b t) -> p b t", t=4),
                     bank[:].rearrange("p (t b) -> p b t", t=4),
                 )
-            quantise(dcodes, dscales, B * g2 + 128 * j0, 256, dgrp[:].rearrange("p h c -> p (h c)"))
+            quantise(dcodes, dscales, B * g2 + 128 * j0, 256, dgrp[:].rearrange("p h c -> p (h c)"), ("D", g2, j0))
 
         def abs_mu(h):
             nc.vector.tensor_single_scalar(
@@ -193,18 +193,11 @@ def tile_pinnlayer_pa_kernel(tc, Volt, IM, Ybr, n_o_mu_i_u, out):
             )
 
         def sum_neg_mu(j):
-            if SMIN[j] == "V":
-                junk_b = epi.tile([P, L], BF16, name="junk_b", bufs=1)
-                nc.vector.tensor_scalar(
-                    out=junk_b[:], in0=mu_sb[:, j, :], scalar1=0.0, scalar2=None,
-                    op0=ALU.min, op1=ALU.add, accum_out=negmu_v[:, j:j + 1],
-                )
-            else:
-                junk_s = epi.tile([P, L], F32, name="junk_s", bufs=1)
-                nc.scalar.activation(
-                    out=junk_s[:], in_=mu_sb[:, j, :], func=ACT.Relu, scale=-1.0,
-                    accum_out=negmu_s[:, j:j + 1],
-                )
+            junk_b = epi.tile([P, L], BF16, name="junk_b", bufs=1)
+            nc.vector.tensor_scalar(
+                out=junk_b[:], in0=mu_sb[:, j, :], scalar1=0.0, scalar2=None,
+                op0=ALU.min, op1=ALU.add, accum_out=negmu_v[:, j:j + 1],
+            )
 
         ys = {}
 
@@ -295,12 +288,10 @@ def tile_pinnlayer_pa_kernel(tc, Volt, IM, Ybr, n_o_mu_i_u, out):
         nc.vector.tensor_scalar(
             out=base[:], in0=negmu_v[:], scalar1=-1.0, scalar2=-0.5 * L, op0=ALU.mult, op1=ALU.add,
         )
-        base2 = keep.tile([P, JB], F32, name="base2")
-        nc.vector.tensor_add(out=base2[:], in0=base[:], in1=negmu_s[:])
         rv = keep.tile([P, JB], F32, name="rv")
         nc.vector.tensor_reduce(out=rv[:], in_=acc_v[:], axis=AX.X, op=ALU.add)
         pre = keep.tile([P, JB], F32, name="pre")
-        nc.vector.tensor_add(out=pre[:], in0=rv[:], in1=base2[:])
+        nc.vector.tensor_add(out=pre[:], in0=rv[:], in1=base[:])
         rs = keep.tile([P, JB], F32, name="rs")
         nc.vector.tensor_reduce(out=rs[:], in_=acc_s[:], axis=AX.X, op=ALU.add)
         res = keep.tile([P, JB], F32, name="res")

@@ -11,291 +11,286 @@ I32 = mybir.dt.int32
 FP8X4 = mybir.dt.float8_e4m3fn_x4
 ALU = mybir.AluOpType
 ACT = mybir.ActivationFunctionType
-AX = mybir.AxisListType
 
 P = 128
+K_PASS = 4 * P
+BANK = 512
 B, N2, L2, L = 1024, 1024, 1536, 768
-JB = B // P
+SAMPLE_TILES = B // P
+PASSES_1 = N2 // K_PASS
+PASSES_2 = L2 // K_PASS
+IM_PAIRS = L2 // (2 * P)
+YBR_TILES = L2 // P
+BANKS_2 = L2 // BANK
+TILE_WORDS = PASSES_1 * P
 FLOPS = 2 * B * N2 * L2 + 2 * B * L2 * L2
-PIN = True
-EV = "SVVSVSSVSSVSSVSSSVSVSSSSSVSSSVSSSVSSSVSSSSVSSVSSVSSSSSSVSSSSVS"
-ABS = "SVSSSSV"
-ABS_LAST = "SSS"
-SEQ = (
-    ("I", 0), ("I", 1), ("V", 0), ("V", 1), ("V", 2), ("V", 3), ("S", 0, 0), ("S", 0, 2),
-    ("I", 2), ("I", 3), ("S", 0, 4), ("S", 0, 6), ("m", 2), ("a", 0), ("I", 4), ("I", 5),
-    ("S", 1, 0), ("S", 1, 2), ("m", 0), ("Y", 0, 0), ("Y", 0, 1), ("Y", 0, 2), ("S", 1, 4), ("S", 1, 6),
-    ("Y", 1, 0), ("m", 1), ("Y", 1, 1), ("Y", 1, 2), ("S", 2, 0), ("S", 2, 2), ("Y", 2, 0), ("Y", 2, 1),
-    ("Y", 2, 2), ("S", 2, 4), ("m", 3), ("a", 1), ("m", 7), ("S", 2, 6), ("m", 4), ("m", 5),
-    ("Z", 0), ("Z", 1), ("Z", 2), ("r", 0), ("r", 1), ("Z", 3), ("r", 2), ("Z", 4),
-    ("Z", 5), ("Z", 6), ("m", 6), ("r", 4), ("r", 5), ("r", 3), ("r", 6), ("Z", 7),
-)
 
 
 def tile_pinnlayer_pa_kernel(tc, Volt, IM, Ybr, n_o_mu_i_u, out):
     nc = tc.nc
     with ExitStack() as ctx:
-        if PIN:
-            ctx.enter_context(tc.manual_schedule())
+        ctx.enter_context(tc.manual_schedule())
         keep = ctx.enter_context(tc.tile_pool(name="keep", bufs=1))
         stage = ctx.enter_context(tc.tile_pool(name="stage", bufs=3))
-        epi = ctx.enter_context(tc.tile_pool(name="epi", bufs=2))
+        epilogue = ctx.enter_context(tc.tile_pool(name="epilogue", bufs=3))
         psum = ctx.enter_context(tc.psum_pool(name="psum", bufs=8))
 
-        ident = keep.tile([P, P], F32, name="ident")
-        make_identity(nc, ident[:])
+        identity = keep.tile([P, P], F32, name="identity")
+        make_identity(nc, identity[:])
 
-        volt_sb = keep.tile([P, JB, N2], BF16, name="volt_sb")
-        im_sb = keep.tile([P, 6, 2, N2], BF16, name="im_sb")
-        ybr_sb = keep.tile([P, 12, L2], BF16, name="ybr_sb")
-        mu_sb = keep.tile([P, JB, L], BF16, name="mu_sb")
-        a_sb = keep.tile([P, JB, L], BF16, name="a_sb")
+        volt_sb = keep.tile([P, SAMPLE_TILES, N2], BF16, name="volt_sb")
+        im_sb = keep.tile([P, IM_PAIRS, 2, N2], BF16, name="im_sb")
+        ybr_sb = keep.tile([P, YBR_TILES, L2], BF16, name="ybr_sb")
+        mu_sb = keep.tile([P, SAMPLE_TILES, L], BF16, name="mu_sb")
+        abs_mu_sb = keep.tile([P, SAMPLE_TILES, L], BF16, name="abs_mu_sb")
 
-        vcodes = keep.tile([P, JB * 256], U32, name="vcodes", align_bytes=64)
-        vscales = keep.tile([P, JB * 256], U8, name="vscales", align_bytes=64)
-        icodes = keep.tile([P, 12 * 256], U32, name="icodes", align_bytes=64)
-        iscales = keep.tile([P, 12 * 256], U8, name="iscales", align_bytes=64)
-        ycodes = keep.tile([P, 3 * L2], U32, name="ycodes", align_bytes=64)
-        yscales = keep.tile([P, 3 * L2], U8, name="yscales", align_bytes=64)
-        dcodes = keep.tile([P, 3 * B], U32, name="dcodes", align_bytes=64)
-        dscales = keep.tile([P, 3 * B], U8, name="dscales", align_bytes=64)
+        volt_codes = keep.tile([P, SAMPLE_TILES * TILE_WORDS], U32, name="volt_codes", align_bytes=64)
+        volt_scales = keep.tile([P, SAMPLE_TILES * TILE_WORDS], U8, name="volt_scales", align_bytes=64)
+        im_codes = keep.tile([P, 2 * IM_PAIRS * TILE_WORDS], U32, name="im_codes", align_bytes=64)
+        im_scales = keep.tile([P, 2 * IM_PAIRS * TILE_WORDS], U8, name="im_scales", align_bytes=64)
+        ybr_codes = keep.tile([P, PASSES_2 * L2], U32, name="ybr_codes", align_bytes=64)
+        ybr_scales = keep.tile([P, PASSES_2 * L2], U8, name="ybr_scales", align_bytes=64)
+        dv_codes = keep.tile([P, PASSES_2 * B], U32, name="dv_codes", align_bytes=64)
+        dv_scales = keep.tile([P, PASSES_2 * B], U8, name="dv_scales", align_bytes=64)
 
-        acc_s = keep.tile([P, JB, 6], F32, name="acc_s")
-        acc_v = keep.tile([P, JB, 3], F32, name="acc_v")
-        negmu_v = keep.tile([P, JB], F32, name="negmu_v")
-        warm = keep.tile([P, 1], F32, name="warm")
-        nc.vector.memset(warm[:], 0.0)
-        nc.vector.memset(acc_s[:], 0.0)
-        nc.vector.memset(acc_v[:], 0.0)
-        nc.scalar.activation(out=warm[:], in_=warm[:], func=ACT.Abs)
+        sums_scalar = keep.tile([P, SAMPLE_TILES, 2 * BANKS_2], F32, name="sums_scalar")
+        sums_vector = keep.tile([P, SAMPLE_TILES], F32, name="sums_vector")
+        min_mu_sums = keep.tile([P, SAMPLE_TILES], F32, name="min_mu_sums")
+        first_abs = keep.tile([P, 1], F32, name="first_abs")
+        nc.vector.memset(first_abs[:], 0.0)
+        nc.vector.memset(sums_scalar[:], 0.0)
+        nc.vector.memset(sums_vector[:], 0.0)
+        nc.scalar.activation(out=first_abs[:], in_=first_abs[:], func=ACT.Abs)
 
-        volt_v = Volt.rearrange("(p j) k -> p j k", j=JB)
-        im_v = IM.rearrange("(t p e) k -> p t e k", t=6, e=2)
-        ybr_v = Ybr.rearrange("(r p) k -> p r k", p=P)
-        mu_v = n_o_mu_i_u.rearrange("(p j) l -> p j l", j=JB)
+        volt_rows = Volt.rearrange("(p j) k -> p j k", j=SAMPLE_TILES)
+        im_rows = IM.rearrange("(t p e) k -> p t e k", t=IM_PAIRS, e=2)
+        ybr_rows = Ybr.rearrange("(r p) k -> p r k", p=P)
+        mu_rows = n_o_mu_i_u.rearrange("(p j) l -> p j l", j=SAMPLE_TILES)
 
-        def load_im(t):
-            nc.sync.dma_start(out=im_sb[:, t, :, :], in_=im_v[:, t, :, :])
+        def load_im(pair):
+            nc.sync.dma_start(out=im_sb[:, pair, :, :], in_=im_rows[:, pair, :, :])
 
-        def load_volt(c):
-            nc.sync.dma_start(out=volt_sb[:, 2 * c:2 * c + 2, :], in_=volt_v[:, 2 * c:2 * c + 2, :])
+        def load_volt(pair):
+            nc.sync.dma_start(out=volt_sb[:, 2 * pair:2 * pair + 2, :], in_=volt_rows[:, 2 * pair:2 * pair + 2, :])
 
-        def load_ybr(rp):
-            nc.sync.dma_start(out=ybr_sb[:, 2 * rp:2 * rp + 2, :], in_=ybr_v[:, 2 * rp:2 * rp + 2, :])
+        def load_ybr(pair):
+            nc.sync.dma_start(out=ybr_sb[:, 2 * pair:2 * pair + 2, :], in_=ybr_rows[:, 2 * pair:2 * pair + 2, :])
+
+        def load_mu(half):
+            nc.sync.dma_start(out=mu_sb[:, 4 * half:4 * half + 4, :], in_=mu_rows[:, 4 * half:4 * half + 4, :])
 
         load_im(0)
         load_im(1)
-        for c in range(4):
-            load_volt(c)
-        for t in range(2, 6):
-            load_im(t)
-        def load_mu(h):
-            nc.sync.dma_start(out=mu_sb[:, 4 * h:4 * h + 4, :], in_=mu_v[:, 4 * h:4 * h + 4, :])
-
+        for pair in range(SAMPLE_TILES // 2):
+            load_volt(pair)
+        for pair in range(2, IM_PAIRS):
+            load_im(pair)
         load_mu(0)
-        for rp in (0, 3, 1, 4, 2, 5):
-            load_ybr(rp)
+        for c in range(BANKS_2):
+            load_ybr(c)
+            load_ybr(BANKS_2 + c)
         load_mu(1)
 
-        volt_w = volt_sb[:].bitcast(F32)
-        im_w = im_sb[:].bitcast(F32)
-        ybr_w = ybr_sb[:].bitcast(F32)
+        volt_words = volt_sb[:].bitcast(F32)
+        im_words = im_sb[:].bitcast(F32)
+        ybr_words = ybr_sb[:].bitcast(F32)
 
-        late = []
-        mark = {"done": 0, "ev": 0}
+        quantises = []
+        written = {"quantises": 0, "copies": 0}
 
-        def flush(upto):
-            for k in range(mark["done"], upto):
-                late[k]()
-            mark["done"] = max(mark["done"], upto)
+        def write_quantises(hold_back):
+            for k in range(written["quantises"], len(quantises) - hold_back):
+                quantises[k]()
+            written["quantises"] = max(written["quantises"], len(quantises) - hold_back)
 
-        def evac(dst, src):
-            eng = EV[mark["ev"]]
-            mark["ev"] += 1
-            if eng == "V":
+        def copy_out(dst, src):
+            if written["copies"] % 4 == 1:
                 nc.vector.tensor_copy(out=dst, in_=src)
             else:
                 nc.scalar.copy(out=dst, in_=src)
+            written["copies"] += 1
 
-        written = set()
-
-        def quantise(codes, scales, lo, words, src, key):
-            def go():
+        def quantise_later(codes, scales, first, words, src):
+            def write():
                 nc.vector.quantize_mx(
-                    out=codes[:, lo:lo + words].bitcast(FP8X4),
-                    scales=scales[:, lo:lo + words],
+                    out=codes[:, first:first + words].bitcast(FP8X4),
+                    scales=scales[:, first:first + words],
                     in_=src,
                 )
-                written.add(key)
-            late.append(go)
-            flush(len(late) - 1)
+            quantises.append(write)
+            write_quantises(1)
 
-        def transposes(srcs, codes, scales, lo, key):
-            grouped = stage.tile([P, 2, 1024], BF16, name="grouped", align_bytes=64)
-            gw = grouped[:].bitcast(F32)
+        def transpose_and_quantise(blocks, codes, scales, first):
+            grouped = stage.tile([P, 2, 4 * 2 * P], BF16, name="grouped", align_bytes=64)
+            grouped_words = grouped[:].bitcast(F32)
             for h in range(2):
-                bank = psum.tile([P, 512], F32, name="bank")
+                bank = psum.tile([P, BANK], F32, name="bank")
                 for q in range(4):
-                    nc.tensor.transpose(bank[:, 128 * q:128 * q + 128], srcs[h][q], ident[:])
-                evac(
-                    gw[:, h, :].rearrange("p (s r u) -> p s r u", s=2, u=2),
+                    nc.tensor.transpose(bank[:, P * q:P * q + P], blocks[h][q], identity[:])
+                copy_out(
+                    grouped_words[:, h, :].rearrange("p (s r u) -> p s r u", s=2, u=2),
                     bank[:].rearrange("p (s u r) -> p s r u", s=2, u=2),
                 )
-            quantise(codes, scales, lo, 512, grouped[:].rearrange("p h c -> p (h c)"), key)
+            quantise_later(codes, scales, first, 4 * P, grouped[:].rearrange("p h c -> p (h c)"))
 
-        def t_volt(c):
-            srcs = [[volt_w[:, 2 * c + h, 128 * q:128 * q + 128] for q in range(4)] for h in range(2)]
-            transposes(srcs, vcodes, vscales, 512 * c, ("V", c))
+        def transpose_volt(pair):
+            blocks = [[volt_words[:, 2 * pair + h, P * q:P * q + P] for q in range(4)] for h in range(2)]
+            transpose_and_quantise(blocks, volt_codes, volt_scales, 2 * TILE_WORDS * pair)
 
-        def t_im(t):
-            srcs = [[im_w[:, t, h, 128 * q:128 * q + 128] for q in range(4)] for h in range(2)]
-            transposes(srcs, icodes, iscales, 512 * t, ("I", t))
+        def transpose_im(pair):
+            blocks = [[im_words[:, pair, h, P * q:P * q + P] for q in range(4)] for h in range(2)]
+            transpose_and_quantise(blocks, im_codes, im_scales, 2 * TILE_WORDS * pair)
 
-        def t_ybr(c, g):
-            srcs = [
-                [ybr_w[:, 2 * rp + q // 2, 256 * g + 128 * (q % 2):256 * g + 128 * (q % 2) + 128] for q in range(4)]
-                for rp in (c, 3 + c)
+        def transpose_ybr(c, g):
+            blocks = [
+                [ybr_words[:, 2 * pair + s, 2 * P * g + P * u:2 * P * g + P * u + P] for s in range(2) for u in range(2)]
+                for pair in (c, BANKS_2 + c)
             ]
-            transposes(srcs, ycodes, yscales, L2 * g + 512 * c, ("Y", c, g))
+            transpose_and_quantise(blocks, ybr_codes, ybr_scales, L2 * g + BANK * c)
 
         def stage1(g2, j0):
-            if not all(k in written for k in (("I", 2 * g2), ("I", 2 * g2 + 1), ("V", j0 // 2))):
-                flush(len(late))
-            dgrp = stage.tile([P, 2, 512], BF16, name="dgrp", align_bytes=64)
+            dv_grouped = stage.tile([P, 2, 4 * P], BF16, name="dv_grouped", align_bytes=64)
             for h in range(2):
-                j = j0 + h
-                bank = psum.tile([P, 512], F32, name="bank")
+                bank = psum.tile([P, BANK], F32, name="bank")
                 for t in range(4):
-                    for g in range(2):
-                        wi = 256 * (4 * g2 + t) + 128 * g
-                        wv = 256 * j + 128 * g
+                    for g in range(PASSES_1):
+                        wi = TILE_WORDS * (4 * g2 + t) + P * g
+                        wv = TILE_WORDS * (j0 + h) + P * g
                         nc.tensor.matmul_mx(
-                            out=bank[:, 128 * t:128 * t + 128],
-                            lhsT=icodes[:, wi:wi + 128].bitcast(FP8X4),
-                            lhsT_scale=iscales[:, wi:wi + 128],
-                            rhs=vcodes[:, wv:wv + 128].bitcast(FP8X4),
-                            rhs_scale=vscales[:, wv:wv + 128],
+                            out=bank[:, P * t:P * t + P],
+                            lhsT=im_codes[:, wi:wi + P].bitcast(FP8X4),
+                            lhsT_scale=im_scales[:, wi:wi + P],
+                            rhs=volt_codes[:, wv:wv + P].bitcast(FP8X4),
+                            rhs_scale=volt_scales[:, wv:wv + P],
                             start=(g == 0),
-                            stop=(g == 1),
+                            stop=(g == PASSES_1 - 1),
                         )
-                evac(
-                    dgrp[:, h, :].rearrange("p (b t) -> p b t", t=4),
+                copy_out(
+                    dv_grouped[:, h, :].rearrange("p (b t) -> p b t", t=4),
                     bank[:].rearrange("p (t b) -> p b t", t=4),
                 )
-            quantise(dcodes, dscales, B * g2 + 128 * j0, 256, dgrp[:].rearrange("p h c -> p (h c)"), ("D", g2, j0))
+            quantise_later(dv_codes, dv_scales, B * g2 + P * j0, 2 * P, dv_grouped[:].rearrange("p h c -> p (h c)"))
 
-        def abs_mu(h):
+        def abs_mu(half):
             nc.vector.tensor_single_scalar(
-                out=a_sb[:, 4 * h:4 * h + 4, :].bitcast(I32),
-                in_=mu_sb[:, 4 * h:4 * h + 4, :].bitcast(I32),
+                out=abs_mu_sb[:, 4 * half:4 * half + 4, :].bitcast(I32),
+                in_=mu_sb[:, 4 * half:4 * half + 4, :].bitcast(I32),
                 scalar=0x7FFF7FFF,
                 op=ALU.bitwise_and,
             )
 
-        def sum_neg_mu(j):
-            junk_b = epi.tile([P, L], BF16, name="junk_b", bufs=1)
+        def sum_min_mu(j):
+            unused = epilogue.tile([P, L], BF16, name="unused_bf16", bufs=1)
             nc.vector.tensor_scalar(
-                out=junk_b[:], in0=mu_sb[:, j, :], scalar1=0.0, scalar2=None,
-                op0=ALU.min, op1=ALU.add, accum_out=negmu_v[:, j:j + 1],
+                out=unused[:], in0=mu_sb[:, j, :], scalar1=0.0, scalar2=None,
+                op0=ALU.min, op1=ALU.add, accum_out=min_mu_sums[:, j:j + 1],
             )
 
-        ys = {}
+        y_tiles = {}
 
-        def abs_sum(j, lo, hi, eng, col):
-            y = ys[j]
-            if eng == "V":
-                junk_v = epi.tile([P, L], F32, name="junk_v", bufs=1)
-                nc.vector.scalar_tensor_tensor(
-                    out=junk_v[:, lo:hi], in0=y[:, lo:hi], scalar=-1.0, in1=y[:, lo:hi],
-                    op0=ALU.mult, op1=ALU.max, accum_out=acc_v[:, j, col:col + 1],
-                )
-            else:
-                junk_s = epi.tile([P, L], F32, name="junk_s", bufs=1)
-                nc.scalar.activation(
-                    out=junk_s[:, lo:hi], in_=y[:, lo:hi], func=ACT.Abs, scale=2.0,
-                    accum_out=acc_s[:, j, 3 + col:4 + col],
-                )
-
-        def xy(j, sq, x, y, lo, hi):
+        def sum_abs_y_on_vector(j):
+            unused = epilogue.tile([P, L], F32, name="unused_vector", bufs=1)
             nc.vector.scalar_tensor_tensor(
-                out=x[:, lo:hi], in0=sq[:, 0, lo:hi], scalar=-1.0, in1=sq[:, 1, lo:hi],
+                out=unused[:], in0=y_tiles[j][:], scalar=-1.0, in1=y_tiles[j][:],
+                op0=ALU.mult, op1=ALU.max, accum_out=sums_vector[:, j:j + 1],
+            )
+
+        def sum_abs_y_on_scalar(j, lo, hi, column):
+            unused = epilogue.tile([P, L], F32, name="unused_scalar", bufs=1)
+            nc.scalar.activation(
+                out=unused[:, lo:hi], in_=y_tiles[j][:, lo:hi], func=ACT.Abs, scale=2.0,
+                accum_out=sums_scalar[:, j, BANKS_2 + column:BANKS_2 + column + 1],
+            )
+
+        def sum_abs_y(j):
+            if j % 2 == 1:
+                sum_abs_y_on_vector(j)
+            else:
+                sum_abs_y_on_scalar(j, 0, L, 0)
+
+        def x_and_y(j, squares, x, lo, hi):
+            nc.vector.scalar_tensor_tensor(
+                out=x[:, lo:hi], in0=squares[:, 0, lo:hi], scalar=-1.0, in1=squares[:, 1, lo:hi],
                 op0=ALU.add, op1=ALU.add,
             )
             nc.vector.scalar_tensor_tensor(
-                out=y[:, lo:hi], in0=a_sb[:, j, lo:hi], scalar=0.5, in1=x[:, lo:hi],
+                out=y_tiles[j][:, lo:hi], in0=abs_mu_sb[:, j, lo:hi], scalar=0.5, in1=x[:, lo:hi],
                 op0=ALU.add, op1=ALU.mult,
             )
 
         def stage2(j):
-            flush(len(late))
-            last = j == JB - 1
-            sq = epi.tile([P, 2, L], F32, name="sq", bufs=3)
-            x = epi.tile([P, L], F32, name="x")
-            y = epi.tile([P, L], F32, name="y", bufs=4)
-            ys[j] = y
-            for c in range(3):
-                bank = psum.tile([P, 512], F32, name="bank")
-                for g in range(3):
-                    wd = B * g + 128 * j
-                    wy = L2 * g + 512 * c
+            last = j == SAMPLE_TILES - 1
+            squares = epilogue.tile([P, 2, L], F32, name="squares")
+            x = epilogue.tile([P, L], F32, name="x")
+            y_tiles[j] = epilogue.tile([P, L], F32, name="y")
+            lines = BANK // 2
+            for c in range(BANKS_2):
+                bank = psum.tile([P, BANK], F32, name="bank")
+                for g in range(PASSES_2):
+                    wd = B * g + P * j
+                    wy = L2 * g + BANK * c
                     nc.tensor.matmul_mx(
                         out=bank[:],
-                        lhsT=dcodes[:, wd:wd + 128].bitcast(FP8X4),
-                        lhsT_scale=dscales[:, wd:wd + 128],
-                        rhs=ycodes[:, wy:wy + 512].bitcast(FP8X4),
-                        rhs_scale=yscales[:, wy:wy + 512],
+                        lhsT=dv_codes[:, wd:wd + P].bitcast(FP8X4),
+                        lhsT_scale=dv_scales[:, wd:wd + P],
+                        rhs=ybr_codes[:, wy:wy + BANK].bitcast(FP8X4),
+                        rhs_scale=ybr_scales[:, wy:wy + BANK],
                         start=(g == 0),
-                        stop=(g == 2),
+                        stop=(g == PASSES_2 - 1),
                     )
                 nc.scalar.activation(
-                    out=sq[:, :, 256 * c:256 * c + 256],
+                    out=squares[:, :, lines * c:lines * c + lines],
                     in_=bank[:].rearrange("p (a w) -> p a w", a=2),
                     func=ACT.Square,
-                    accum_out=acc_s[:, j, c:c + 1],
+                    accum_out=sums_scalar[:, j, c:c + 1],
                 )
                 if last:
-                    xy(j, sq, x, y, 256 * c, 256 * c + 256)
+                    x_and_y(j, squares, x, lines * c, lines * c + lines)
                     if c > 0:
-                        abs_sum(j, 256 * (c - 1), 256 * c, ABS_LAST[c - 1], c - 1)
+                        sum_abs_y_on_scalar(j, lines * (c - 1), lines * c, c - 1)
             if last:
-                abs_sum(j, 512, 768, ABS_LAST[2], 2)
+                sum_abs_y_on_scalar(j, lines * (BANKS_2 - 1), L, BANKS_2 - 1)
             else:
-                xy(j, sq, x, y, 0, L)
+                x_and_y(j, squares, x, 0, L)
 
-        for tok in SEQ:
-            kind = tok[0]
-            args = tok[1:]
-            if kind == "I":
-                t_im(args[0])
-            elif kind == "V":
-                t_volt(args[0])
-            elif kind == "Y":
-                t_ybr(args[0], args[1])
-            elif kind == "S":
-                stage1(args[0], args[1])
-            elif kind == "F":
-                flush(len(late))
-            elif kind == "a":
-                abs_mu(args[0])
-            elif kind == "m":
-                sum_neg_mu(args[0])
-            elif kind == "Z":
-                stage2(args[0])
-            elif kind == "r":
-                abs_sum(args[0], 0, L, ABS[args[0]], 0)
+        transpose_im(0)
+        transpose_im(1)
+        for pair in range(SAMPLE_TILES // 2):
+            transpose_volt(pair)
+        for n in range(2 * PASSES_2):
+            stage1(n // 2, 4 * (n % 2))
+            stage1(n // 2, 4 * (n % 2) + 2)
+            if n < 2:
+                transpose_im(2 * n + 2)
+                transpose_im(2 * n + 3)
+            elif n < 2 + BANKS_2:
+                for g in range(PASSES_2):
+                    transpose_ybr(n - 2, g)
+            if n == 2:
+                abs_mu(0)
+            if n >= 2:
+                sum_min_mu(n - 2)
+        write_quantises(0)
+        abs_mu(1)
+        for j in range(SAMPLE_TILES - 1):
+            stage2(j)
+            if j > 0:
+                sum_abs_y(j - 1)
+            if j < 4:
+                sum_min_mu(4 + j)
+        sum_abs_y(SAMPLE_TILES - 2)
+        stage2(SAMPLE_TILES - 1)
 
-        base = keep.tile([P, JB], F32, name="base")
-        nc.vector.tensor_scalar(
-            out=base[:], in0=negmu_v[:], scalar1=-1.0, scalar2=-0.5 * L, op0=ALU.mult, op1=ALU.add,
-        )
-        rv = keep.tile([P, JB], F32, name="rv")
-        nc.vector.tensor_reduce(out=rv[:], in_=acc_v[:], axis=AX.X, op=ALU.add)
-        pre = keep.tile([P, JB], F32, name="pre")
-        nc.vector.tensor_add(out=pre[:], in0=rv[:], in1=base[:])
-        rs = keep.tile([P, JB], F32, name="rs")
-        nc.vector.tensor_reduce(out=rs[:], in_=acc_s[:], axis=AX.X, op=ALU.add)
-        res = keep.tile([P, JB], F32, name="res")
+        from_vector = keep.tile([P, SAMPLE_TILES], F32, name="from_vector")
         nc.vector.scalar_tensor_tensor(
-            out=res[:], in0=rs[:], scalar=0.5, in1=pre[:], op0=ALU.mult, op1=ALU.add,
+            out=from_vector[:], in0=min_mu_sums[:], scalar=-1.0, in1=sums_vector[:], op0=ALU.mult, op1=ALU.add,
         )
-        nc.sync.dma_start(out=out.rearrange("(p j) -> p j", j=JB), in_=res[:])
+        ready = keep.tile([P, SAMPLE_TILES], F32, name="ready")
+        nc.vector.tensor_scalar_add(out=ready[:], in0=from_vector[:], scalar1=-0.5 * L)
+        from_scalar = keep.tile([P, SAMPLE_TILES], F32, name="from_scalar")
+        nc.vector.tensor_reduce(out=from_scalar[:], in_=sums_scalar[:], axis=mybir.AxisListType.X, op=ALU.add)
+        result = keep.tile([P, SAMPLE_TILES], F32, name="result")
+        nc.vector.scalar_tensor_tensor(
+            out=result[:], in0=from_scalar[:], scalar=0.5, in1=ready[:], op0=ALU.mult, op1=ALU.add,
+        )
+        nc.sync.dma_start(out=out.rearrange("(p j) -> p j", j=SAMPLE_TILES), in_=result[:])

from contextlib import ExitStack

import concourse.mybir as mybir
from concourse.masks import make_identity

F32 = mybir.dt.float32
BF16 = mybir.dt.bfloat16
U32 = mybir.dt.uint32
U8 = mybir.dt.uint8
I32 = mybir.dt.int32
FP8X4 = mybir.dt.float8_e4m3fn_x4
ALU = mybir.AluOpType
ACT = mybir.ActivationFunctionType

P = 128
K_PASS = 4 * P
BANK = 512
B, N2, L2, L = 1024, 1024, 1536, 768
SAMPLE_TILES = B // P
PASSES_1 = N2 // K_PASS
PASSES_2 = L2 // K_PASS
IM_PAIRS = L2 // (2 * P)
YBR_TILES = L2 // P
BANKS_2 = L2 // BANK
TILE_WORDS = PASSES_1 * P
FLOPS = 2 * B * N2 * L2 + 2 * B * L2 * L2


def tile_pinnlayer_pa_kernel(tc, Volt, IM, Ybr, n_o_mu_i_u, out):
    nc = tc.nc
    with ExitStack() as ctx:
        ctx.enter_context(tc.manual_schedule())
        keep = ctx.enter_context(tc.tile_pool(name="keep", bufs=1))
        stage = ctx.enter_context(tc.tile_pool(name="stage", bufs=3))
        epilogue = ctx.enter_context(tc.tile_pool(name="epilogue", bufs=3))
        psum = ctx.enter_context(tc.psum_pool(name="psum", bufs=8))

        identity = keep.tile([P, P], F32, name="identity")
        make_identity(nc, identity[:])

        volt_sb = keep.tile([P, SAMPLE_TILES, N2], BF16, name="volt_sb")
        im_sb = keep.tile([P, IM_PAIRS, 2, N2], BF16, name="im_sb")
        ybr_sb = keep.tile([P, YBR_TILES, L2], BF16, name="ybr_sb")
        mu_sb = keep.tile([P, SAMPLE_TILES, L], BF16, name="mu_sb")
        abs_mu_sb = keep.tile([P, SAMPLE_TILES, L], BF16, name="abs_mu_sb")

        volt_codes = keep.tile([P, SAMPLE_TILES * TILE_WORDS], U32, name="volt_codes", align_bytes=64)
        volt_scales = keep.tile([P, SAMPLE_TILES * TILE_WORDS], U8, name="volt_scales", align_bytes=64)
        im_codes = keep.tile([P, 2 * IM_PAIRS * TILE_WORDS], U32, name="im_codes", align_bytes=64)
        im_scales = keep.tile([P, 2 * IM_PAIRS * TILE_WORDS], U8, name="im_scales", align_bytes=64)
        ybr_codes = keep.tile([P, PASSES_2 * L2], U32, name="ybr_codes", align_bytes=64)
        ybr_scales = keep.tile([P, PASSES_2 * L2], U8, name="ybr_scales", align_bytes=64)
        dv_codes = keep.tile([P, PASSES_2 * B], U32, name="dv_codes", align_bytes=64)
        dv_scales = keep.tile([P, PASSES_2 * B], U8, name="dv_scales", align_bytes=64)

        sums_scalar = keep.tile([P, SAMPLE_TILES, 2 * BANKS_2], F32, name="sums_scalar")
        sums_vector = keep.tile([P, SAMPLE_TILES], F32, name="sums_vector")
        min_mu_sums = keep.tile([P, SAMPLE_TILES], F32, name="min_mu_sums")
        first_abs = keep.tile([P, 1], F32, name="first_abs")
        nc.vector.memset(first_abs[:], 0.0)
        nc.vector.memset(sums_scalar[:], 0.0)
        nc.vector.memset(sums_vector[:], 0.0)
        nc.scalar.activation(out=first_abs[:], in_=first_abs[:], func=ACT.Abs)

        volt_rows = Volt.rearrange("(p j) k -> p j k", j=SAMPLE_TILES)
        im_rows = IM.rearrange("(t p e) k -> p t e k", t=IM_PAIRS, e=2)
        ybr_rows = Ybr.rearrange("(r p) k -> p r k", p=P)
        mu_rows = n_o_mu_i_u.rearrange("(p j) l -> p j l", j=SAMPLE_TILES)

        def load_im(pair):
            nc.sync.dma_start(out=im_sb[:, pair, :, :], in_=im_rows[:, pair, :, :])

        def load_volt(pair):
            nc.sync.dma_start(out=volt_sb[:, 2 * pair:2 * pair + 2, :], in_=volt_rows[:, 2 * pair:2 * pair + 2, :])

        def load_ybr(pair):
            nc.sync.dma_start(out=ybr_sb[:, 2 * pair:2 * pair + 2, :], in_=ybr_rows[:, 2 * pair:2 * pair + 2, :])

        def load_mu(half):
            nc.sync.dma_start(out=mu_sb[:, 4 * half:4 * half + 4, :], in_=mu_rows[:, 4 * half:4 * half + 4, :])

        load_im(0)
        load_im(1)
        for pair in range(SAMPLE_TILES // 2):
            load_volt(pair)
        for pair in range(2, IM_PAIRS):
            load_im(pair)
        load_mu(0)
        for c in range(BANKS_2):
            load_ybr(c)
            load_ybr(BANKS_2 + c)
        load_mu(1)

        volt_words = volt_sb[:].bitcast(F32)
        im_words = im_sb[:].bitcast(F32)
        ybr_words = ybr_sb[:].bitcast(F32)

        quantises = []
        written = {"quantises": 0, "copies": 0}

        def write_quantises(hold_back):
            for k in range(written["quantises"], len(quantises) - hold_back):
                quantises[k]()
            written["quantises"] = max(written["quantises"], len(quantises) - hold_back)

        def copy_out(dst, src):
            if written["copies"] % 4 == 1:
                nc.vector.tensor_copy(out=dst, in_=src)
            else:
                nc.scalar.copy(out=dst, in_=src)
            written["copies"] += 1

        def quantise_later(codes, scales, first, words, src):
            def write():
                nc.vector.quantize_mx(
                    out=codes[:, first:first + words].bitcast(FP8X4),
                    scales=scales[:, first:first + words],
                    in_=src,
                )
            quantises.append(write)
            write_quantises(1)

        def transpose_and_quantise(blocks, codes, scales, first):
            grouped = stage.tile([P, 2, 4 * 2 * P], BF16, name="grouped", align_bytes=64)
            grouped_words = grouped[:].bitcast(F32)
            for h in range(2):
                bank = psum.tile([P, BANK], F32, name="bank")
                for q in range(4):
                    nc.tensor.transpose(bank[:, P * q:P * q + P], blocks[h][q], identity[:])
                copy_out(
                    grouped_words[:, h, :].rearrange("p (s r u) -> p s r u", s=2, u=2),
                    bank[:].rearrange("p (s u r) -> p s r u", s=2, u=2),
                )
            quantise_later(codes, scales, first, 4 * P, grouped[:].rearrange("p h c -> p (h c)"))

        def transpose_volt(pair):
            blocks = [[volt_words[:, 2 * pair + h, P * q:P * q + P] for q in range(4)] for h in range(2)]
            transpose_and_quantise(blocks, volt_codes, volt_scales, 2 * TILE_WORDS * pair)

        def transpose_im(pair):
            blocks = [[im_words[:, pair, h, P * q:P * q + P] for q in range(4)] for h in range(2)]
            transpose_and_quantise(blocks, im_codes, im_scales, 2 * TILE_WORDS * pair)

        def transpose_ybr(c, g):
            blocks = [
                [ybr_words[:, 2 * pair + s, 2 * P * g + P * u:2 * P * g + P * u + P] for s in range(2) for u in range(2)]
                for pair in (c, BANKS_2 + c)
            ]
            transpose_and_quantise(blocks, ybr_codes, ybr_scales, L2 * g + BANK * c)

        def stage1(g2, j0):
            dv_grouped = stage.tile([P, 2, 4 * P], BF16, name="dv_grouped", align_bytes=64)
            for h in range(2):
                bank = psum.tile([P, BANK], F32, name="bank")
                for t in range(4):
                    for g in range(PASSES_1):
                        wi = TILE_WORDS * (4 * g2 + t) + P * g
                        wv = TILE_WORDS * (j0 + h) + P * g
                        nc.tensor.matmul_mx(
                            out=bank[:, P * t:P * t + P],
                            lhsT=im_codes[:, wi:wi + P].bitcast(FP8X4),
                            lhsT_scale=im_scales[:, wi:wi + P],
                            rhs=volt_codes[:, wv:wv + P].bitcast(FP8X4),
                            rhs_scale=volt_scales[:, wv:wv + P],
                            start=(g == 0),
                            stop=(g == PASSES_1 - 1),
                        )
                copy_out(
                    dv_grouped[:, h, :].rearrange("p (b t) -> p b t", t=4),
                    bank[:].rearrange("p (t b) -> p b t", t=4),
                )
            quantise_later(dv_codes, dv_scales, B * g2 + P * j0, 2 * P, dv_grouped[:].rearrange("p h c -> p (h c)"))

        def abs_mu(half):
            nc.vector.tensor_single_scalar(
                out=abs_mu_sb[:, 4 * half:4 * half + 4, :].bitcast(I32),
                in_=mu_sb[:, 4 * half:4 * half + 4, :].bitcast(I32),
                scalar=0x7FFF7FFF,
                op=ALU.bitwise_and,
            )

        def sum_min_mu(j):
            unused = epilogue.tile([P, L], BF16, name="unused_bf16", bufs=1)
            nc.vector.tensor_scalar(
                out=unused[:], in0=mu_sb[:, j, :], scalar1=0.0, scalar2=None,
                op0=ALU.min, op1=ALU.add, accum_out=min_mu_sums[:, j:j + 1],
            )

        y_tiles = {}

        def sum_abs_y_on_vector(j):
            unused = epilogue.tile([P, L], F32, name="unused_vector", bufs=1)
            nc.vector.scalar_tensor_tensor(
                out=unused[:], in0=y_tiles[j][:], scalar=-1.0, in1=y_tiles[j][:],
                op0=ALU.mult, op1=ALU.max, accum_out=sums_vector[:, j:j + 1],
            )

        def sum_abs_y_on_scalar(j, lo, hi, column):
            unused = epilogue.tile([P, L], F32, name="unused_scalar", bufs=1)
            nc.scalar.activation(
                out=unused[:, lo:hi], in_=y_tiles[j][:, lo:hi], func=ACT.Abs, scale=2.0,
                accum_out=sums_scalar[:, j, BANKS_2 + column:BANKS_2 + column + 1],
            )

        def sum_abs_y(j):
            if j % 2 == 1:
                sum_abs_y_on_vector(j)
            else:
                sum_abs_y_on_scalar(j, 0, L, 0)

        def x_and_y(j, squares, x, lo, hi):
            nc.vector.scalar_tensor_tensor(
                out=x[:, lo:hi], in0=squares[:, 0, lo:hi], scalar=-1.0, in1=squares[:, 1, lo:hi],
                op0=ALU.add, op1=ALU.add,
            )
            nc.vector.scalar_tensor_tensor(
                out=y_tiles[j][:, lo:hi], in0=abs_mu_sb[:, j, lo:hi], scalar=0.5, in1=x[:, lo:hi],
                op0=ALU.add, op1=ALU.mult,
            )

        def stage2(j):
            last = j == SAMPLE_TILES - 1
            squares = epilogue.tile([P, 2, L], F32, name="squares")
            x = epilogue.tile([P, L], F32, name="x")
            y_tiles[j] = epilogue.tile([P, L], F32, name="y")
            lines = BANK // 2
            for c in range(BANKS_2):
                bank = psum.tile([P, BANK], F32, name="bank")
                for g in range(PASSES_2):
                    wd = B * g + P * j
                    wy = L2 * g + BANK * c
                    nc.tensor.matmul_mx(
                        out=bank[:],
                        lhsT=dv_codes[:, wd:wd + P].bitcast(FP8X4),
                        lhsT_scale=dv_scales[:, wd:wd + P],
                        rhs=ybr_codes[:, wy:wy + BANK].bitcast(FP8X4),
                        rhs_scale=ybr_scales[:, wy:wy + BANK],
                        start=(g == 0),
                        stop=(g == PASSES_2 - 1),
                    )
                nc.scalar.activation(
                    out=squares[:, :, lines * c:lines * c + lines],
                    in_=bank[:].rearrange("p (a w) -> p a w", a=2),
                    func=ACT.Square,
                    accum_out=sums_scalar[:, j, c:c + 1],
                )
                if last:
                    x_and_y(j, squares, x, lines * c, lines * c + lines)
                    if c > 0:
                        sum_abs_y_on_scalar(j, lines * (c - 1), lines * c, c - 1)
            if last:
                sum_abs_y_on_scalar(j, lines * (BANKS_2 - 1), L, BANKS_2 - 1)
            else:
                x_and_y(j, squares, x, 0, L)

        transpose_im(0)
        transpose_im(1)
        for pair in range(SAMPLE_TILES // 2):
            transpose_volt(pair)
        for n in range(2 * PASSES_2):
            stage1(n // 2, 4 * (n % 2))
            stage1(n // 2, 4 * (n % 2) + 2)
            if n < 2:
                transpose_im(2 * n + 2)
                transpose_im(2 * n + 3)
            elif n < 2 + BANKS_2:
                for g in range(PASSES_2):
                    transpose_ybr(n - 2, g)
            if n == 2:
                abs_mu(0)
            if n >= 2:
                sum_min_mu(n - 2)
        write_quantises(0)
        abs_mu(1)
        for j in range(SAMPLE_TILES - 1):
            stage2(j)
            if j > 0:
                sum_abs_y(j - 1)
            if j < 4:
                sum_min_mu(4 + j)
        sum_abs_y(SAMPLE_TILES - 2)
        stage2(SAMPLE_TILES - 1)

        from_vector = keep.tile([P, SAMPLE_TILES], F32, name="from_vector")
        nc.vector.scalar_tensor_tensor(
            out=from_vector[:], in0=min_mu_sums[:], scalar=-1.0, in1=sums_vector[:], op0=ALU.mult, op1=ALU.add,
        )
        ready = keep.tile([P, SAMPLE_TILES], F32, name="ready")
        nc.vector.tensor_scalar_add(out=ready[:], in0=from_vector[:], scalar1=-0.5 * L)
        from_scalar = keep.tile([P, SAMPLE_TILES], F32, name="from_scalar")
        nc.vector.tensor_reduce(out=from_scalar[:], in_=sums_scalar[:], axis=mybir.AxisListType.X, op=ALU.add)
        result = keep.tile([P, SAMPLE_TILES], F32, name="result")
        nc.vector.scalar_tensor_tensor(
            out=result[:], in0=from_scalar[:], scalar=0.5, in1=ready[:], op0=ALU.mult, op1=ALU.add,
        )
        nc.sync.dma_start(out=out.rearrange("(p j) -> p j", j=SAMPLE_TILES), in_=result[:])
